import numpy as np
import ml_dtypes


def mxq(x, axis, fmt="e4m3"):
    dtype, down = {"e4m3": (ml_dtypes.float8_e4m3fn, 7), "e5m2": (ml_dtypes.float8_e5m2, 14)}[fmt]
    v = np.moveaxis(np.asarray(x, np.float32).astype(ml_dtypes.bfloat16).astype(np.float64), axis, -1)
    blocks = v.reshape(v.shape[:-1] + (-1, 32))
    amax = np.abs(blocks).max(-1, keepdims=True)
    byte = np.maximum(np.where(amax > 0, np.frexp(amax)[1] - 1 + 127, 0) - down, 1)
    scale = np.exp2(byte - 127.0)
    codes = (blocks / scale).astype(np.float32).astype(dtype).astype(np.float64)
    return np.moveaxis((codes * scale).reshape(v.shape), -1, axis)


WIDE = False


def mx_kscale(k):
    if not WIDE:
        return np.ones(k)
    levels = np.array([10, -10, 5, -5, 0])
    if k % 512:
        return np.exp2(np.random.permutation(np.resize(levels, k // 32))).repeat(32)
    a = np.empty((k // 512, 16))
    for p in range(k // 512):
        a[p, :8] = np.random.permutation(np.resize(levels, 8))
        for g in range(8):
            far = levels[np.abs(levels - a[p, g]) >= 10]
            a[p, g + 8] = far[np.random.randint(len(far))]
    return np.exp2(a.ravel()).repeat(32)


BF16 = ml_dtypes.bfloat16


def bf(x):
    return np.asarray(x, np.float32).astype(BF16)


def f64(x):
    return np.asarray(x).astype(np.float64)


B, H, W, C, NF, ZD = 128, 8, 8, 512, 256, 512
EPS = 1e-8
LRELU_SLOPE = 0.2


def setup_inputs():
    s = mx_kscale(C)
    return {"x": bf(np.random.standard_normal((B, H, W, C)) * s),
            "dlatents": bf(np.random.standard_normal((B, ZD))),
            "noise_map": bf(np.random.standard_normal((B, H, W, 1))),
            "conv_w": bf(np.random.standard_normal((C, NF)) / np.sqrt(C) / s[:, None]),
            "noise_weight": bf(np.random.standard_normal((1, 1, 1, NF)) * 0.5),
            "bias": bf(np.random.standard_normal((1, 1, 1, NF)) * 0.5),
            "dense_w": bf(np.random.standard_normal((ZD, 2 * NF)) / np.sqrt(ZD)),
            "dense_b": bf(np.random.standard_normal(2 * NF) * 0.3)}


def reference(x, dlatents, noise_map, conv_w, noise_weight, bias, dense_w, dense_b):
    y = mxq(f64(x), 3, "e4m3") @ mxq(f64(conv_w), 0, "e4m3")
    y = y + f64(noise_weight) * f64(noise_map) + f64(bias)
    y = np.where(y >= 0.0, y, LRELU_SLOPE * y)
    mu = np.mean(y, axis=(1, 2), keepdims=True)
    var = np.mean(np.square(y - mu), axis=(1, 2), keepdims=True)
    yn = (y - mu) / np.sqrt(var + EPS)
    gb = f64(dlatents) @ f64(dense_w) + f64(dense_b)
    nf = y.shape[-1]
    gb = gb.reshape(-1, 2, 1, 1, nf)
    gamma, beta = gb[:, 0], gb[:, 1]
    return yn * (1.0 + gamma) + beta

@@ -1,0 +1,369 @@
+from contextlib import ExitStack
+
+import concourse.mybir as mybir
+from concourse.masks import make_identity
+
+F32 = mybir.dt.float32
+BF16 = mybir.dt.bfloat16
+U32 = mybir.dt.uint32
+U8 = mybir.dt.uint8
+FP8X4 = mybir.dt.float8_e4m3fn_x4
+ALU = mybir.AluOpType
+ACT = mybir.ActivationFunctionType
+
+P = 128
+PIX = 8192
+CIN = 512
+NF = 256
+GP = 512
+NG = PIX // GP
+EPS = 1e-8
+SLOPE = 0.2
+FLOPS = 2 * PIX * CIN * NF + 2 * 128 * 512 * 512
+
+
+def tile_styleganlayerepilogue_t_kernel(
+    tc, x, dlatents, noise_map, conv_w, noise_weight, bias, dense_w, dense_b, out
+):
+    nc = tc.nc
+    x_rows = x.rearrange("b h w k -> (b h w) k")
+    out_rows = out.rearrange("b h w c -> (b h w) c")
+    nm_flat = noise_map.rearrange("b h w o -> (b h w o)")
+
+    with ExitStack() as ctx:
+        ctx.enter_context(tc.manual_schedule())
+        const = ctx.enter_context(tc.tile_pool(name="const", bufs=1))
+        xpool = ctx.enter_context(tc.tile_pool(name="xpool", bufs=NG))
+        mpool = ctx.enter_context(tc.tile_pool(name="mpool", bufs=NG))
+        gpool = ctx.enter_context(tc.tile_pool(name="gpool", bufs=3))
+        spool = ctx.enter_context(tc.tile_pool(name="spool", bufs=5))
+        opool = ctx.enter_context(tc.tile_pool(name="opool", bufs=3))
+        psx = ctx.enter_context(tc.psum_pool(name="psx", bufs=2))
+        psp = ctx.enter_context(tc.psum_pool(name="psp", bufs=4))
+        pso = ctx.enter_context(tc.psum_pool(name="pso", bufs=2))
+
+        ident_f = const.tile([P, P], F32, name="ident_f")
+        make_identity(nc, ident_f[:])
+        eps_t = const.tile([P, 1], F32, name="eps_t")
+        nc.vector.memset(eps_t[:], EPS)
+        vrows = const.tile([P, P], BF16, name="vrows")
+        nc.vector.memset(vrows[:], 0.0)
+        warm = const.tile([P, 1], F32, name="warm")
+        nc.scalar.activation(out=warm[:], in_=eps_t[:], func=ACT.Abs_reciprocal_sqrt)
+        ident_b = const.tile([P, P], BF16, name="ident_b")
+        nc.vector.tensor_copy(out=ident_b[:], in_=ident_f[:])
+
+        x_sb = []
+
+        def load_x(g):
+            t = xpool.tile([P, 4 * CIN], BF16, name="x_sb")
+            nc.sync.dma_start(
+                out=t[:],
+                in_=x_rows[GP * g : GP * (g + 1), :].rearrange("(p j) k -> p (j k)", j=4),
+            )
+            x_sb.append(t)
+
+        nm_t = []
+
+        def load_nm(q):
+            t = const.tile([P, 2048], BF16, name="nm%d" % q)
+            nc.sync.dma_start(
+                out=t[:], in_=nm_flat[2048 * q : 2048 * (q + 1)].partition_broadcast(P)
+            )
+            nm_t.append(t)
+
+        load_x(0)
+        nc.sync.dma_start(
+            out=vrows[0:2, :], in_=noise_weight.rearrange("a b c (h n) -> (a b c h) n", h=2)
+        )
+        nc.sync.dma_start(out=vrows[2:4, :], in_=bias.rearrange("a b c (h n) -> (a b c h) n", h=2))
+        nc.sync.dma_start(out=vrows[4:8, :], in_=dense_b.rearrange("(h n) -> h n", h=4))
+        w_raw = const.tile([P, 4 * NF], BF16, name="w_raw")
+        nc.sync.dma_start(out=w_raw[:], in_=conv_w.rearrange("(i t) c -> i (t c)", t=4))
+        load_nm(0)
+        load_x(1)
+        load_x(2)
+        dl_sb = const.tile([P, 512], BF16, name="dl_sb")
+        nc.sync.dma_start(out=dl_sb[:], in_=dlatents)
+        dw_sb = const.tile([P, 2048], BF16, name="dw_sb")
+        nc.sync.dma_start(
+            out=dw_sb[:].rearrange("p (kb n) -> p kb n", kb=4),
+            in_=dense_w.rearrange("(kb p) n -> p kb n", p=P),
+        )
+        load_x(3)
+        load_nm(1)
+        load_x(4)
+        load_x(5)
+        load_nm(2)
+        load_x(6)
+        load_x(7)
+        load_nm(3)
+        for g in range(8, NG):
+            load_x(g)
+
+        vps = pso.tile([P, P], BF16, name="vps", tag="ot")
+        nc.tensor.transpose(vps[:], vrows[:], ident_b[:])
+        vec = const.tile([P, 8], F32, name="vec")
+        nc.vector.tensor_copy(out=vec[:], in_=vps[:, 0:8])
+        one_g = const.tile([P, 2], F32, name="one_g")
+        nc.vector.tensor_scalar_add(out=one_g[:], in0=vec[:, 4:6], scalar1=1.0)
+
+        w_grp = const.tile([P, 4 * NF], BF16, name="w_grp", align_bytes=64)
+        nc.vector.tensor_copy(
+            out=w_grp[:].rearrange("i (c t) -> i c t", t=4),
+            in_=w_raw[:].rearrange("i (t c) -> i c t", t=4),
+        )
+        w_codes = const.tile([P, NF], U32, name="w_codes", align_bytes=64)
+        w_scl = const.tile([P, NF], U8, name="w_scl", align_bytes=64)
+        nc.vector.quantize_mx(out=w_codes[:].bitcast(FP8X4), scales=w_scl[:], in_=w_grp[:])
+
+        m_sb = {}
+
+        def noise(g):
+            t = mpool.tile([P, 2 * GP], F32, name="m_sb")
+            src = nm_t[g // 4][:, GP * (g % 4) : GP * (g % 4 + 1)].rearrange("c (p j) -> c j p", j=4)
+            for h in range(2):
+                nc.gpsimd.tensor_scalar(
+                    out=t[:, GP * h : GP * (h + 1)].rearrange("c (j p) -> c j p", j=4),
+                    in0=src,
+                    scalar1=vec[:, h : h + 1],
+                    scalar2=vec[:, 2 + h : 3 + h],
+                    op0=ALU.mult,
+                    op1=ALU.add,
+                )
+            m_sb[g] = t
+
+        g1 = const.tile([P, 2 * P], F32, name="g1")
+        bt = const.tile([P, 2 * P], F32, name="bt")
+        dl_t = const.tile([P, 512], BF16, name="dl_t")
+        style_ps = {}
+
+        def style_transposes():
+            dl_ps = pso.tile([P, 512], BF16, name="dl_ps", tag="ot")
+            for kb in range(4):
+                nc.tensor.transpose(
+                    dl_ps[:, P * kb : P * (kb + 1)], dl_sb[:, P * kb : P * (kb + 1)], ident_b[:]
+                )
+            style_ps["dl"] = dl_ps
+
+        def style_copy():
+            nc.vector.tensor_copy(out=dl_t[:], in_=style_ps["dl"][:])
+
+        def style_matmuls():
+            gb = pso.tile([P, 512], F32, name="gb", tag="ot")
+            for cb in range(4):
+                for kb in range(4):
+                    nc.tensor.matmul(
+                        out=gb[:, P * cb : P * (cb + 1)],
+                        lhsT=dw_sb[:, 512 * kb + P * cb : 512 * kb + P * (cb + 1)],
+                        rhs=dl_t[:, P * kb : P * (kb + 1)],
+                        start=(kb == 0),
+                        stop=(kb == 3),
+                    )
+            g1v = g1[:].rearrange("c (g h s) -> c h g s", h=2, s=8)
+            btv = bt[:].rearrange("c (g h s) -> c h g s", h=2, s=8)
+            for h in range(2):
+                nc.scalar.activation(
+                    out=g1v[:, h],
+                    in_=gb[:, P * h : P * (h + 1)].rearrange("c (g s) -> c g s", s=8),
+                    func=ACT.Identity,
+                    bias=one_g[:, h : h + 1],
+                )
+                nc.scalar.activation(
+                    out=btv[:, h],
+                    in_=gb[:, P * (2 + h) : P * (3 + h)].rearrange("c (g s) -> c g s", s=8),
+                    func=ACT.Identity,
+                    bias=vec[:, 6 + h : 7 + h],
+                )
+
+        xts = {}
+        grp = {}
+        prod = {}
+        stats = {}
+        rstd = {}
+        coef = {}
+
+        def t_in(g):
+            x32 = x_sb[g][:].bitcast(F32)
+            banks = []
+            for jj in range(2):
+                xt = psx.tile([P, 512], F32, name="xt")
+                for u in range(2):
+                    for j2 in range(2):
+                        j = 2 * jj + j2
+                        nc.tensor.transpose(
+                            xt[:, 256 * u + P * j2 : 256 * u + P * (j2 + 1)],
+                            x32[:, 256 * j + u : 256 * (j + 1) : 2],
+                            ident_f[:],
+                        )
+                banks.append(xt)
+            xts[g] = banks
+
+        def x_out(g):
+            t = gpool.tile([P, 4 * GP], BF16, name="grp", align_bytes=64)
+            t32 = t[:].bitcast(F32)
+            for jj in range(2):
+                nc.scalar.copy(
+                    out=t32[:, 512 * jj : 512 * (jj + 1)].rearrange("p (c u) -> p c u", u=2),
+                    in_=xts[g][jj][:].rearrange("p (u c) -> p c u", u=2),
+                )
+            grp[g] = t
+
+        def quant_mx(g):
+            cd = gpool.tile([P, GP], U32, name="codes", align_bytes=64)
+            sc = gpool.tile([P, GP], U8, name="scl", align_bytes=64)
+            nc.vector.quantize_mx(out=cd[:].bitcast(FP8X4), scales=sc[:], in_=grp[g][:])
+            pp = []
+            for h in range(2):
+                acc = psp.tile([P, GP], F32, name="acc")
+                nc.tensor.matmul_mx(
+                    out=acc[:],
+                    lhsT=w_codes[:, P * h : P * (h + 1)].bitcast(FP8X4),
+                    lhsT_scale=w_scl[:, P * h : P * (h + 1)],
+                    rhs=cd[:].bitcast(FP8X4),
+                    rhs_scale=sc[:],
+                    start=True,
+                    stop=True,
+                )
+                pp.append(acc)
+            prod[g] = pp
+
+        def add_noise(g):
+            t = m_sb[g]
+            for h in range(2):
+                nc.vector.tensor_tensor(
+                    out=t[:, GP * h : GP * (h + 1)],
+                    in0=prod[g][h][:],
+                    in1=t[:, GP * h : GP * (h + 1)],
+                    op=ALU.add,
+                )
+
+        def lrelu(g):
+            t = m_sb[g]
+            for h in range(2):
+                th = t[:, GP * h : GP * (h + 1)]
+                nc.vector.scalar_tensor_tensor(
+                    out=th, in0=th, scalar=SLOPE, in1=th, op0=ALU.mult, op1=ALU.max
+                )
+
+        def moments(g):
+            t = m_sb[g]
+            st = spool.tile([P, 48], F32, name="st")
+            for h in range(2):
+                yv = t[:, GP * h : GP * (h + 1)].rearrange(
+                    "c (j sp s2 q) -> c sp j q s2", j=4, sp=4, s2=2, q=16
+                )
+                for sp in range(4):
+                    idx = h * 4 + sp
+                    nc.vector.bn_stats(out=st[:, 6 * idx : 6 * idx + 6], in_=yv[:, sp])
+            stats[g] = st
+
+        def inv_std(g):
+            st3 = stats[g][:].rearrange("c (n k) -> c n k", k=3)
+            rs = spool.tile([P, 16], F32, name="rs")
+            nc.scalar.activation(
+                out=rs[:],
+                in_=st3[:, :, 2],
+                func=ACT.Abs_reciprocal_sqrt,
+                scale=1.0 / 64.0,
+                bias=eps_t[:],
+            )
+            rstd[g] = rs
+
+        def coefficients(g, eng):
+            st3 = stats[g][:].rearrange("c (n k) -> c n k", k=3)
+            a_t = spool.tile([P, 16], F32, name="a_t")
+            eng.tensor_tensor(
+                out=a_t[:], in0=rstd[g][:], in1=g1[:, 16 * g : 16 * (g + 1)], op=ALU.mult
+            )
+            ma = spool.tile([P, 16], F32, name="ma")
+            eng.tensor_tensor(out=ma[:], in0=st3[:, :, 1], in1=a_t[:], op=ALU.mult)
+            b_t = spool.tile([P, 16], F32, name="b_t")
+            eng.tensor_tensor(
+                out=b_t[:], in0=bt[:, 16 * g : 16 * (g + 1)], in1=ma[:], op=ALU.subtract
+            )
+            coef[g] = (a_t, b_t)
+
+        def back(g, split):
+            a_t, b_t = coef[g]
+            t = m_sb[g]
+            for h in range(2):
+                yv = t[:, GP * h : GP * (h + 1)].rearrange("c (j s q) -> c s j q", j=4, s=8, q=16)
+                for s in range(8):
+                    lc = 8 * h + s
+                    if split and h == 1:
+                        nc.vector.tensor_scalar(
+                            out=yv[:, s],
+                            in0=yv[:, s],
+                            scalar1=a_t[:, lc : lc + 1],
+                            scalar2=b_t[:, lc : lc + 1],
+                            op0=ALU.mult,
+                            op1=ALU.add,
+                        )
+                    else:
+                        nc.scalar.activation(
+                            out=yv[:, s],
+                            in_=yv[:, s],
+                            func=ACT.Identity,
+                            scale=a_t[:, lc : lc + 1],
+                            bias=b_t[:, lc : lc + 1],
+                        )
+            o_sb = opool.tile([P, 4 * NF], F32, name="o_sb")
+            ov = o_sb[:].rearrange("p (j c) -> p j c", c=NF)
+            banks = []
+            for h in range(2):
+                ot = pso.tile([P, 512], F32, name="ot")
+                for j in range(4):
+                    nc.tensor.transpose(
+                        ot[:, P * j : P * (j + 1)],
+                        t[:, GP * h + P * j : GP * h + P * (j + 1)],
+                        ident_f[:],
+                    )
+                banks.append(ot)
+            for h in range(2):
+                dst = ov[:, :, P * h : P * (h + 1)]
+                src = banks[h][:].rearrange("p (j c) -> p j c", c=P)
+                if split and h == 1:
+                    nc.vector.tensor_copy(out=dst, in_=src)
+                else:
+                    nc.scalar.copy(out=dst, in_=src)
+            nc.sync.dma_start(
+                out=out_rows[GP * g : GP * (g + 1), :].rearrange("(p j) c -> p (j c)", j=4),
+                in_=o_sb[:],
+            )
+
+        for g in range(4):
+            noise(g)
+        t_in(0)
+        x_out(0)
+        t_in(1)
+        x_out(1)
+        quant_mx(0)
+        t_in(2)
+        for i in range(NG + 2):
+            if i + 2 < NG:
+                x_out(i + 2)
+            if i < NG:
+                add_noise(i)
+            if i + 1 < NG:
+                quant_mx(i + 1)
+            if i == 0:
+                style_transposes()
+            if i == 1:
+                style_matmuls()
+            if i < NG:
+                lrelu(i)
+            if i == 0:
+                style_copy()
+            if 1 <= i <= NG:
+                coefficients(i - 1, nc.vector if i == NG else nc.gpsimd)
+            if i + 4 < NG:
+                noise(i + 4)
+            if i < NG:
+                moments(i)
+            if i >= 2:
+                back(i - 2, i >= NG)
+            if i + 3 < NG:
+                t_in(i + 3)
+            if i < NG:
+                inv_std(i)

@@ -39,15 +39,16 @@ def tile_styleganlayerepilogue_t_kernel(
         spool = ctx.enter_context(tc.tile_pool(name="spool", bufs=5))
         opool = ctx.enter_context(tc.tile_pool(name="opool", bufs=3))
         psx = ctx.enter_context(tc.psum_pool(name="psx", bufs=2))
-        psp = ctx.enter_context(tc.psum_pool(name="psp", bufs=4))
+        psp = ctx.enter_context(tc.psum_pool(name="psp", bufs=3))
+        psn = ctx.enter_context(tc.psum_pool(name="psn", bufs=1))
         pso = ctx.enter_context(tc.psum_pool(name="pso", bufs=2))
 
         ident_f = const.tile([P, P], F32, name="ident_f")
         make_identity(nc, ident_f[:])
         eps_t = const.tile([P, 1], F32, name="eps_t")
         nc.vector.memset(eps_t[:], EPS)
-        vrows = const.tile([P, P], BF16, name="vrows")
-        nc.vector.memset(vrows[:], 0.0)
+        rows = const.tile([P, GP], BF16, name="rows")
+        nc.vector.memset(rows[:], 0.0)
         warm = const.tile([P, 1], F32, name="warm")
         nc.scalar.activation(out=warm[:], in_=eps_t[:], func=ACT.Abs_reciprocal_sqrt)
         ident_b = const.tile([P, P], BF16, name="ident_b")
@@ -63,24 +64,13 @@ def tile_styleganlayerepilogue_t_kernel(
             )
             x_sb.append(t)
 
-        nm_t = []
-
-        def load_nm(q):
-            t = const.tile([P, 2048], BF16, name="nm%d" % q)
-            nc.sync.dma_start(
-                out=t[:], in_=nm_flat[2048 * q : 2048 * (q + 1)].partition_broadcast(P)
-            )
-            nm_t.append(t)
-
         load_x(0)
-        nc.sync.dma_start(
-            out=vrows[0:2, :], in_=noise_weight.rearrange("a b c (h n) -> (a b c h) n", h=2)
-        )
-        nc.sync.dma_start(out=vrows[2:4, :], in_=bias.rearrange("a b c (h n) -> (a b c h) n", h=2))
-        nc.sync.dma_start(out=vrows[4:8, :], in_=dense_b.rearrange("(h n) -> h n", h=4))
+        nc.sync.dma_start(out=rows[0:NG, :], in_=nm_flat.rearrange("(g n) -> g n", n=GP))
+        nc.sync.dma_start(out=rows[16:17, 0:NF], in_=noise_weight.rearrange("a b c n -> (a b c) n"))
+        nc.sync.dma_start(out=rows[16:17, NF : 2 * NF], in_=bias.rearrange("a b c n -> (a b c) n"))
+        nc.sync.dma_start(out=rows[17:18, :], in_=dense_b.rearrange("(o n) -> o n", o=1))
         w_raw = const.tile([P, 4 * NF], BF16, name="w_raw")
         nc.sync.dma_start(out=w_raw[:], in_=conv_w.rearrange("(i t) c -> i (t c)", t=4))
-        load_nm(0)
         load_x(1)
         load_x(2)
         dl_sb = const.tile([P, 512], BF16, name="dl_sb")
@@ -91,43 +81,66 @@ def tile_styleganlayerepilogue_t_kernel(
             in_=dense_w.rearrange("(kb p) n -> p kb n", p=P),
         )
         load_x(3)
-        load_nm(1)
         load_x(4)
         load_x(5)
-        load_nm(2)
         load_x(6)
         load_x(7)
-        load_nm(3)
         for g in range(8, NG):
             load_x(g)
 
-        vps = pso.tile([P, P], BF16, name="vps", tag="ot")
-        nc.tensor.transpose(vps[:], vrows[:], ident_b[:])
-        vec = const.tile([P, 8], F32, name="vec")
-        nc.vector.tensor_copy(out=vec[:], in_=vps[:, 0:8])
-        one_g = const.tile([P, 2], F32, name="one_g")
-        nc.vector.tensor_scalar_add(out=one_g[:], in0=vec[:, 4:6], scalar1=1.0)
-
         w_grp = const.tile([P, 4 * NF], BF16, name="w_grp", align_bytes=64)
-        nc.vector.tensor_copy(
-            out=w_grp[:].rearrange("i (c t) -> i c t", t=4),
-            in_=w_raw[:].rearrange("i (t c) -> i c t", t=4),
-        )
         w_codes = const.tile([P, NF], U32, name="w_codes", align_bytes=64)
         w_scl = const.tile([P, NF], U8, name="w_scl", align_bytes=64)
-        nc.vector.quantize_mx(out=w_codes[:].bitcast(FP8X4), scales=w_scl[:], in_=w_grp[:])
+
+        def quant_w():
+            nc.vector.tensor_copy(
+                out=w_grp[:].rearrange("i (c t) -> i c t", t=4),
+                in_=w_raw[:].rearrange("i (t c) -> i c t", t=4),
+            )
+            nc.vector.quantize_mx(out=w_codes[:].bitcast(FP8X4), scales=w_scl[:], in_=w_grp[:])
+
+        vec = const.tile([P, 8], F32, name="vec")
+        vec3 = vec[:].rearrange("c (b r) -> c b r", r=2)
+        one_g = const.tile([P, 2], F32, name="one_g")
+        nm_pix = const.tile([P, 4, NG], BF16, name="nm_pix")
+
+        def vectors():
+            nps = pso.tile([P, 4, P], BF16, name="nps", tag="ot")
+            vps = pso.tile([P, 4, P], BF16, name="vps", tag="ot")
+            for j in range(4):
+                nc.tensor.transpose(nps[:, j, :], rows[:, j:GP:4], ident_b[:])
+            for b in range(4):
+                nc.tensor.transpose(vps[:, b, :], rows[:, P * b : P * (b + 1)], ident_b[:])
+            nc.vector.tensor_copy(out=nm_pix[:], in_=nps[:, :, 0:NG])
+            nc.vector.tensor_copy(out=vec3, in_=vps[:, :, 16:18])
+            nc.vector.tensor_scalar_add(out=one_g[:], in0=vec3[:, 0:2, 1], scalar1=1.0)
+
+        nm_bc = {}
+
+        def spread_noise(q, eng_copy):
+            nb = psn.tile([P, 2 * GP], BF16, name="nb")
+            for e in range(2):
+                for j in range(4):
+                    nc.tensor.transpose(
+                        nb[:, GP * e + P * j : GP * e + P * (j + 1)],
+                        nm_pix[:, j, 2 * q + e : 2 * q + e + 1].to_broadcast([P, P]),
+                        ident_b[:],
+                    )
+            t = const.tile([P, 2 * GP], BF16, name="nm_bc%d" % q)
+            eng_copy(out=t[:], in_=nb[:])
+            nm_bc[q] = t
 
         m_sb = {}
 
         def noise(g):
             t = mpool.tile([P, 2 * GP], F32, name="m_sb")
-            src = nm_t[g // 4][:, GP * (g % 4) : GP * (g % 4 + 1)].rearrange("c (p j) -> c j p", j=4)
+            src = nm_bc[g // 2][:, GP * (g % 2) : GP * (g % 2 + 1)]
             for h in range(2):
                 nc.gpsimd.tensor_scalar(
-                    out=t[:, GP * h : GP * (h + 1)].rearrange("c (j p) -> c j p", j=4),
+                    out=t[:, GP * h : GP * (h + 1)],
                     in0=src,
-                    scalar1=vec[:, h : h + 1],
-                    scalar2=vec[:, 2 + h : 3 + h],
+                    scalar1=vec3[:, h, 0:1],
+                    scalar2=vec3[:, 2 + h, 0:1],
                     op0=ALU.mult,
                     op1=ALU.add,
                 )
@@ -173,7 +186,7 @@ def tile_styleganlayerepilogue_t_kernel(
                     out=btv[:, h],
                     in_=gb[:, P * (2 + h) : P * (3 + h)].rearrange("c (g s) -> c g s", s=8),
                     func=ACT.Identity,
-                    bias=vec[:, 6 + h : 7 + h],
+                    bias=vec3[:, 2 + h, 1:2],
                 )
 
         xts = {}
@@ -332,14 +345,21 @@ def tile_styleganlayerepilogue_t_kernel(
                 in_=o_sb[:],
             )
 
-        for g in range(4):
-            noise(g)
         t_in(0)
         x_out(0)
+        vectors()
+        spread_noise(0, nc.vector.tensor_copy)
+        noise(0)
+        noise(1)
+        quant_w()
         t_in(1)
         x_out(1)
         quant_mx(0)
+        spread_noise(1, nc.vector.tensor_copy)
+        noise(2)
+        noise(3)
         t_in(2)
+        spread_noise(2, nc.vector.tensor_copy)
         for i in range(NG + 2):
             if i + 2 < NG:
                 x_out(i + 2)
@@ -347,6 +367,8 @@ def tile_styleganlayerepilogue_t_kernel(
                 add_noise(i)
             if i + 1 < NG:
                 quant_mx(i + 1)
+            if i + 3 < NG // 2:
+                spread_noise(i + 3, nc.scalar.copy)
             if i == 0:
                 style_transposes()
             if i == 1:

@@ -34,7 +34,8 @@ def tile_styleganlayerepilogue_t_kernel(
         ctx.enter_context(tc.manual_schedule())
         const = ctx.enter_context(tc.tile_pool(name="const", bufs=1))
         xpool = ctx.enter_context(tc.tile_pool(name="xpool", bufs=NG))
-        mpool = ctx.enter_context(tc.tile_pool(name="mpool", bufs=NG))
+        npool = ctx.enter_context(tc.tile_pool(name="npool", bufs=2))
+        ypool = ctx.enter_context(tc.tile_pool(name="ypool", bufs=4))
         gpool = ctx.enter_context(tc.tile_pool(name="gpool", bufs=3))
         spool = ctx.enter_context(tc.tile_pool(name="spool", bufs=5))
         opool = ctx.enter_context(tc.tile_pool(name="opool", bufs=3))
@@ -64,7 +65,12 @@ def tile_styleganlayerepilogue_t_kernel(
             )
             x_sb.append(t)
 
-        load_x(0)
+        x_0 = xpool.tile([P, 4 * CIN], BF16, name="x_sb")
+        x_rows_0 = x_rows[0:GP, :].rearrange("(p j) k -> p (j k)", j=4)
+        for jj in range(2):
+            cols = slice(2 * CIN * jj, 2 * CIN * (jj + 1))
+            nc.sync.dma_start(out=x_0[:, cols], in_=x_rows_0[:, cols])
+        x_sb.append(x_0)
         nc.sync.dma_start(out=rows[0:NG, :], in_=nm_flat.rearrange("(g n) -> g n", n=GP))
         nc.sync.dma_start(out=rows[16:17, 0:NF], in_=noise_weight.rearrange("a b c n -> (a b c) n"))
         nc.sync.dma_start(out=rows[16:17, NF : 2 * NF], in_=bias.rearrange("a b c n -> (a b c) n"))
@@ -80,12 +86,7 @@ def tile_styleganlayerepilogue_t_kernel(
             out=dw_sb[:].rearrange("p (kb n) -> p kb n", kb=4),
             in_=dense_w.rearrange("(kb p) n -> p kb n", p=P),
         )
-        load_x(3)
-        load_x(4)
-        load_x(5)
-        load_x(6)
-        load_x(7)
-        for g in range(8, NG):
+        for g in range(3, NG):
             load_x(g)
 
         w_grp = const.tile([P, 4 * NF], BF16, name="w_grp", align_bytes=64)
@@ -102,49 +103,72 @@ def tile_styleganlayerepilogue_t_kernel(
         vec = const.tile([P, 8], F32, name="vec")
         vec3 = vec[:].rearrange("c (b r) -> c b r", r=2)
         one_g = const.tile([P, 2], F32, name="one_g")
-        nm_pix = const.tile([P, 4, NG], BF16, name="nm_pix")
+        nm_pix = const.tile([P, 2, NG], F32, name="nm_pix")
 
         def vectors():
-            nps = pso.tile([P, 4, P], BF16, name="nps", tag="ot")
+            nps = pso.tile([P, 2, P], F32, name="nps", tag="ot")
             vps = pso.tile([P, 4, P], BF16, name="vps", tag="ot")
-            for j in range(4):
-                nc.tensor.transpose(nps[:, j, :], rows[:, j:GP:4], ident_b[:])
+            rows_32 = rows[:].bitcast(F32)
+            for jj in range(2):
+                nc.tensor.transpose(nps[:, jj, :], rows_32[:, jj : GP // 2 : 2], ident_f[:])
             for b in range(4):
                 nc.tensor.transpose(vps[:, b, :], rows[:, P * b : P * (b + 1)], ident_b[:])
-            nc.vector.tensor_copy(out=nm_pix[:], in_=nps[:, :, 0:NG])
+            nc.scalar.copy(out=nm_pix[:], in_=nps[:, :, 0:NG])
             nc.vector.tensor_copy(out=vec3, in_=vps[:, :, 16:18])
-            nc.vector.tensor_scalar_add(out=one_g[:], in0=vec3[:, 0:2, 1], scalar1=1.0)
 
+        nm_ps = {}
         nm_bc = {}
 
-        def spread_noise(q, eng_copy):
-            nb = psn.tile([P, 2 * GP], BF16, name="nb")
+        def spread_noise(q, pool, tag):
+            nb = pool.tile([P, GP], F32, name="nb", tag=tag)
             for e in range(2):
-                for j in range(4):
+                for jj in range(2):
+                    lo = 256 * e + P * jj
                     nc.tensor.transpose(
-                        nb[:, GP * e + P * j : GP * e + P * (j + 1)],
-                        nm_pix[:, j, 2 * q + e : 2 * q + e + 1].to_broadcast([P, P]),
-                        ident_b[:],
+                        nb[:, lo : lo + P],
+                        nm_pix[:, jj, 2 * q + e : 2 * q + e + 1].to_broadcast([P, P]),
+                        ident_f[:],
                     )
-            t = const.tile([P, 2 * GP], BF16, name="nm_bc%d" % q)
-            eng_copy(out=t[:], in_=nb[:])
+            nm_ps[q] = nb
+
+        def keep_noise(q, eng_copy, lo=0):
+            t = const.tile([P, GP], F32, name="nm_bc%d" % q)
+            eng_copy(out=t[:, lo:GP], in_=nm_ps[q][:, lo:GP])
             nm_bc[q] = t
 
-        m_sb = {}
+        n_sb = {}
+        y_sb = {}
+
+        def noise_0(h, engine):
+            if h == 0:
+                n_sb[0] = npool.tile([P, 2 * GP], F32, name="n_sb")
+            dst = n_sb[0][:, GP * h : GP * (h + 1)].rearrange("c (jj e p) -> c jj e p", jj=2, e=2)
+            src = nm_ps[0][:].bitcast(BF16)[:, 0:GP].rearrange("c (jj p e) -> c jj e p", jj=2, e=2)
+            w_col, b_col = vec3[:, h, 0:1], vec3[:, 2 + h, 0:1]
+            if engine == "vector":
+                nc.vector.tensor_scalar(
+                    out=dst, in0=src, scalar1=w_col, scalar2=b_col, op0=ALU.mult, op1=ALU.add
+                )
+            else:
+                nc.scalar.activation(
+                    out=dst, in_=src, func=ACT.Identity, scale=w_col, bias=b_col
+                )
 
         def noise(g):
-            t = mpool.tile([P, 2 * GP], F32, name="m_sb")
-            src = nm_bc[g // 2][:, GP * (g % 2) : GP * (g % 2 + 1)]
+            t = npool.tile([P, 2 * GP], F32, name="n_sb")
+            src = nm_bc[g // 2][:].bitcast(BF16)[:, GP * (g % 2) : GP * (g % 2 + 1)].rearrange(
+                "c (jj p e) -> c jj e p", jj=2, e=2
+            )
             for h in range(2):
                 nc.gpsimd.tensor_scalar(
-                    out=t[:, GP * h : GP * (h + 1)],
+                    out=t[:, GP * h : GP * (h + 1)].rearrange("c (jj e p) -> c jj e p", jj=2, e=2),
                     in0=src,
                     scalar1=vec3[:, h, 0:1],
                     scalar2=vec3[:, 2 + h, 0:1],
                     op0=ALU.mult,
                     op1=ALU.add,
                 )
-            m_sb[g] = t
+            n_sb[g] = t
 
         g1 = const.tile([P, 2 * P], F32, name="g1")
         bt = const.tile([P, 2 * P], F32, name="bt")
@@ -191,15 +215,17 @@ def tile_styleganlayerepilogue_t_kernel(
 
         xts = {}
         grp = {}
+        codes = {}
         prod = {}
+        outs = {}
+        o_sb = {}
         stats = {}
         rstd = {}
         coef = {}
 
-        def t_in(g):
+        def t_in(g, parts=(0, 1)):
             x32 = x_sb[g][:].bitcast(F32)
-            banks = []
-            for jj in range(2):
+            for jj in parts:
                 xt = psx.tile([P, 512], F32, name="xt")
                 for u in range(2):
                     for j2 in range(2):
@@ -209,8 +235,7 @@ def tile_styleganlayerepilogue_t_kernel(
                             x32[:, 256 * j + u : 256 * (j + 1) : 2],
                             ident_f[:],
                         )
-                banks.append(xt)
-            xts[g] = banks
+                xts[g, jj] = xt
 
         def x_out(g):
             t = gpool.tile([P, 4 * GP], BF16, name="grp", align_bytes=64)
@@ -218,15 +243,18 @@ def tile_styleganlayerepilogue_t_kernel(
             for jj in range(2):
                 nc.scalar.copy(
                     out=t32[:, 512 * jj : 512 * (jj + 1)].rearrange("p (c u) -> p c u", u=2),
-                    in_=xts[g][jj][:].rearrange("p (u c) -> p c u", u=2),
+                    in_=xts[g, jj][:].rearrange("p (u c) -> p c u", u=2),
                 )
             grp[g] = t
 
-        def quant_mx(g):
+        def quant(g):
             cd = gpool.tile([P, GP], U32, name="codes", align_bytes=64)
             sc = gpool.tile([P, GP], U8, name="scl", align_bytes=64)
             nc.vector.quantize_mx(out=cd[:].bitcast(FP8X4), scales=sc[:], in_=grp[g][:])
-            pp = []
+            codes[g] = (cd, sc)
+
+        def products(g):
+            cd, sc = codes[g]
             for h in range(2):
                 acc = psp.tile([P, GP], F32, name="acc")
                 nc.tensor.matmul_mx(
@@ -238,154 +266,193 @@ def tile_styleganlayerepilogue_t_kernel(
                     start=True,
                     stop=True,
                 )
-                pp.append(acc)
-            prod[g] = pp
+                prod[g, h] = acc
 
         def add_noise(g):
-            t = m_sb[g]
+            t = ypool.tile([P, 2 * GP], F32, name="y_sb")
             for h in range(2):
                 nc.vector.tensor_tensor(
                     out=t[:, GP * h : GP * (h + 1)],
-                    in0=prod[g][h][:],
-                    in1=t[:, GP * h : GP * (h + 1)],
+                    in0=prod[g, h][:],
+                    in1=n_sb[g][:, GP * h : GP * (h + 1)],
                     op=ALU.add,
                 )
+            y_sb[g] = t
 
         def lrelu(g):
-            t = m_sb[g]
             for h in range(2):
-                th = t[:, GP * h : GP * (h + 1)]
+                th = y_sb[g][:, GP * h : GP * (h + 1)]
                 nc.vector.scalar_tensor_tensor(
                     out=th, in0=th, scalar=SLOPE, in1=th, op0=ALU.mult, op1=ALU.max
                 )
 
-        def moments(g):
-            t = m_sb[g]
-            st = spool.tile([P, 48], F32, name="st")
-            for h in range(2):
-                yv = t[:, GP * h : GP * (h + 1)].rearrange(
+        def moments(g, halves=(0, 1)):
+            if g not in stats:
+                stats[g] = spool.tile([P, 48], F32, name="st")
+            st = stats[g]
+            for h in halves:
+                yv = y_sb[g][:, GP * h : GP * (h + 1)].rearrange(
                     "c (j sp s2 q) -> c sp j q s2", j=4, sp=4, s2=2, q=16
                 )
                 for sp in range(4):
                     idx = h * 4 + sp
                     nc.vector.bn_stats(out=st[:, 6 * idx : 6 * idx + 6], in_=yv[:, sp])
-            stats[g] = st
 
-        def inv_std(g):
+        def inv_std(g, lo=0, hi=16):
             st3 = stats[g][:].rearrange("c (n k) -> c n k", k=3)
-            rs = spool.tile([P, 16], F32, name="rs")
+            if g not in rstd:
+                rstd[g] = spool.tile([P, 16], F32, name="rs")
             nc.scalar.activation(
-                out=rs[:],
-                in_=st3[:, :, 2],
+                out=rstd[g][:, lo:hi],
+                in_=st3[:, lo:hi, 2],
                 func=ACT.Abs_reciprocal_sqrt,
                 scale=1.0 / 64.0,
                 bias=eps_t[:],
             )
-            rstd[g] = rs
 
-        def coefficients(g, eng):
+        def coefficients(g, eng, lo=0, hi=16):
             st3 = stats[g][:].rearrange("c (n k) -> c n k", k=3)
-            a_t = spool.tile([P, 16], F32, name="a_t")
-            eng.tensor_tensor(
-                out=a_t[:], in0=rstd[g][:], in1=g1[:, 16 * g : 16 * (g + 1)], op=ALU.mult
-            )
-            ma = spool.tile([P, 16], F32, name="ma")
-            eng.tensor_tensor(out=ma[:], in0=st3[:, :, 1], in1=a_t[:], op=ALU.mult)
-            b_t = spool.tile([P, 16], F32, name="b_t")
-            eng.tensor_tensor(
-                out=b_t[:], in0=bt[:, 16 * g : 16 * (g + 1)], in1=ma[:], op=ALU.subtract
-            )
-            coef[g] = (a_t, b_t)
+            if g not in coef:
+                a_t = spool.tile([P, 16], F32, name="a_t")
+                b_t = spool.tile([P, 16], F32, name="b_t")
+                ma = spool.tile([P, 16], F32, name="ma")
+                coef[g] = (a_t, b_t, ma)
+            a_t, b_t, ma = coef[g]
+            cols = slice(16 * g + lo, 16 * g + hi)
+            eng.tensor_tensor(out=a_t[:, lo:hi], in0=rstd[g][:, lo:hi], in1=g1[:, cols], op=ALU.mult)
+            eng.tensor_tensor(out=ma[:, lo:hi], in0=st3[:, lo:hi, 1], in1=a_t[:, lo:hi], op=ALU.mult)
+            eng.tensor_tensor(out=b_t[:, lo:hi], in0=bt[:, cols], in1=ma[:, lo:hi], op=ALU.subtract)
 
-        def back(g, split):
-            a_t, b_t = coef[g]
-            t = m_sb[g]
-            for h in range(2):
-                yv = t[:, GP * h : GP * (h + 1)].rearrange("c (j s q) -> c s j q", j=4, s=8, q=16)
-                for s in range(8):
-                    lc = 8 * h + s
-                    if split and h == 1:
-                        nc.vector.tensor_scalar(
-                            out=yv[:, s],
-                            in0=yv[:, s],
-                            scalar1=a_t[:, lc : lc + 1],
-                            scalar2=b_t[:, lc : lc + 1],
-                            op0=ALU.mult,
-                            op1=ALU.add,
-                        )
-                    else:
-                        nc.scalar.activation(
-                            out=yv[:, s],
-                            in_=yv[:, s],
-                            func=ACT.Identity,
-                            scale=a_t[:, lc : lc + 1],
-                            bias=b_t[:, lc : lc + 1],
-                        )
-            o_sb = opool.tile([P, 4 * NF], F32, name="o_sb")
-            ov = o_sb[:].rearrange("p (j c) -> p j c", c=NF)
-            banks = []
-            for h in range(2):
-                ot = pso.tile([P, 512], F32, name="ot")
-                for j in range(4):
-                    nc.tensor.transpose(
-                        ot[:, P * j : P * (j + 1)],
-                        t[:, GP * h + P * j : GP * h + P * (j + 1)],
-                        ident_f[:],
+        def affine(g, h, on_vector):
+            a_t, b_t, ma = coef[g]
+            yv = y_sb[g][:, GP * h : GP * (h + 1)].rearrange("c (j s q) -> c s j q", j=4, s=8, q=16)
+            for s in range(8):
+                lc = 8 * h + s
+                if on_vector:
+                    nc.vector.tensor_scalar(
+                        out=yv[:, s],
+                        in0=yv[:, s],
+                        scalar1=a_t[:, lc : lc + 1],
+                        scalar2=b_t[:, lc : lc + 1],
+                        op0=ALU.mult,
+                        op1=ALU.add,
                     )
-                banks.append(ot)
-            for h in range(2):
-                dst = ov[:, :, P * h : P * (h + 1)]
-                src = banks[h][:].rearrange("p (j c) -> p j c", c=P)
-                if split and h == 1:
-                    nc.vector.tensor_copy(out=dst, in_=src)
                 else:
-                    nc.scalar.copy(out=dst, in_=src)
+                    nc.scalar.activation(
+                        out=yv[:, s],
+                        in_=yv[:, s],
+                        func=ACT.Identity,
+                        scale=a_t[:, lc : lc + 1],
+                        bias=b_t[:, lc : lc + 1],
+                    )
+
+        def t_back(g, h):
+            ot = pso.tile([P, 512], F32, name="ot")
+            for j in range(4):
+                nc.tensor.transpose(
+                    ot[:, P * j : P * (j + 1)],
+                    y_sb[g][:, GP * h + P * j : GP * h + P * (j + 1)],
+                    ident_f[:],
+                )
+            outs[g, h] = ot
+
+        def copy_out(g, h, eng_copy):
+            if g not in o_sb:
+                o_sb[g] = opool.tile([P, 4 * NF], F32, name="o_sb")
+            ov = o_sb[g][:].rearrange("p (j c) -> p j c", c=NF)
+            eng_copy(
+                out=ov[:, :, P * h : P * (h + 1)],
+                in_=outs[g, h][:].rearrange("p (j c) -> p j c", c=P),
+            )
+
+        def store(g):
             nc.sync.dma_start(
                 out=out_rows[GP * g : GP * (g + 1), :].rearrange("(p j) c -> p (j c)", j=4),
-                in_=o_sb[:],
+                in_=o_sb[g][:],
             )
+
+        def store_half(g, h):
+            ov = o_sb[g][:].rearrange("p (j c) -> p j c", c=NF)
+            dst = out_rows[GP * g : GP * (g + 1), :].rearrange("(p j) c -> p j c", j=4)
+            cols = slice(P * h, P * (h + 1))
+            nc.sync.dma_start(out=dst[:, :, cols], in_=ov[:, :, cols])
 
         t_in(0)
         x_out(0)
-        vectors()
-        spread_noise(0, nc.vector.tensor_copy)
-        noise(0)
-        noise(1)
         quant_w()
-        t_in(1)
+        vectors()
+        quant(0)
+        spread_noise(0, psn, "nb")
+        noise_0(0, "vector")
+        noise_0(1, "scalar")
+        t_in(1, (0,))
+        products(0)
+        t_in(1, (1,))
         x_out(1)
-        quant_mx(0)
-        spread_noise(1, nc.vector.tensor_copy)
-        noise(2)
-        noise(3)
         t_in(2)
-        spread_noise(2, nc.vector.tensor_copy)
-        for i in range(NG + 2):
+        add_noise(0)
+        keep_noise(0, nc.vector.tensor_copy, GP // 2)
+        nc.vector.tensor_scalar_add(out=one_g[:], in0=vec3[:, 0:2, 1], scalar1=1.0)
+        noise(1)
+        for i in range(NG):
+            if i + 1 < NG:
+                quant(i + 1)
+                products(i + 1)
+            if i >= 3 and i < NG - 1:
+                copy_out(i - 3, 0, nc.scalar.copy)
+                copy_out(i - 3, 1, nc.scalar.copy)
+                store(i - 3)
             if i + 2 < NG:
                 x_out(i + 2)
-            if i < NG:
+            if i >= 1:
                 add_noise(i)
-            if i + 1 < NG:
-                quant_mx(i + 1)
-            if i + 3 < NG // 2:
-                spread_noise(i + 3, nc.scalar.copy)
+            if i + 3 < NG:
+                t_in(i + 3)
+            if i < 3:
+                for q in range(3 * i + 1, min(3 * i + 4, NG // 2)):
+                    spread_noise(q, *((psn, "nb") if q % 2 else (pso, "ot")))
+                    keep_noise(q, nc.scalar.copy)
+            if i + 2 < NG:
+                noise(i + 2)
+            if i >= 2:
+                affine(i - 2, 0, False)
+                t_back(i - 2, 0)
+                affine(i - 2, 1, False)
+                t_back(i - 2, 1)
+            if i >= 1:
+                moments(i - 1)
             if i == 0:
                 style_transposes()
             if i == 1:
-                style_matmuls()
-            if i < NG:
-                lrelu(i)
-            if i == 0:
                 style_copy()
-            if 1 <= i <= NG:
-                coefficients(i - 1, nc.vector if i == NG else nc.gpsimd)
-            if i + 4 < NG:
-                noise(i + 4)
-            if i < NG:
-                moments(i)
-            if i >= 2:
-                back(i - 2, i >= NG)
-            if i + 3 < NG:
-                t_in(i + 3)
-            if i < NG:
-                inv_std(i)
+                style_matmuls()
+            lrelu(i)
+            if i >= NG - 2:
+                copy_out(i - 2, 0, nc.scalar.copy)
+                copy_out(i - 2, 1, nc.scalar.copy)
+                store(i - 2)
+            if i >= 1:
+                inv_std(i - 1)
+                coefficients(i - 1, nc.gpsimd)
+        g, z = NG - 2, NG - 1
+        moments(z, (0,))
+        affine(g, 0, False)
+        t_back(g, 0)
+        inv_std(z, 0, 8)
+        coefficients(z, nc.gpsimd, 0, 8)
+        moments(z, (1,))
+        affine(g, 1, True)
+        t_back(g, 1)
+        inv_std(z, 8, 16)
+        copy_out(g, 0, nc.scalar.copy)
+        coefficients(z, nc.vector, 8, 16)
+        affine(z, 0, False)
+        affine(z, 1, True)
+        copy_out(g, 1, nc.scalar.copy)
+        store(g)
+        t_back(z, 0)
+        t_back(z, 1)
+        copy_out(z, 0, nc.scalar.copy)
+        copy_out(z, 1, nc.vector.tensor_copy)
+        store_half(z, 0)
+        store_half(z, 1)

@@ -19,6 +19,7 @@ GP = 512
 NG = PIX // GP
 EPS = 1e-8
 SLOPE = 0.2
+N_SCALAR = 12
 FLOPS = 2 * PIX * CIN * NF + 2 * 128 * 512 * 512
 
 
@@ -117,58 +118,32 @@ def tile_styleganlayerepilogue_t_kernel(
             nc.vector.tensor_copy(out=vec3, in_=vps[:, :, 16:18])
 
         nm_ps = {}
-        nm_bc = {}
 
-        def spread_noise(q, pool, tag):
-            nb = pool.tile([P, GP], F32, name="nb", tag=tag)
-            for e in range(2):
-                for jj in range(2):
-                    lo = 256 * e + P * jj
-                    nc.tensor.transpose(
-                        nb[:, lo : lo + P],
-                        nm_pix[:, jj, 2 * q + e : 2 * q + e + 1].to_broadcast([P, P]),
-                        ident_f[:],
-                    )
-            nm_ps[q] = nb
-
-        def keep_noise(q, eng_copy, lo=0):
-            t = const.tile([P, GP], F32, name="nm_bc%d" % q)
-            eng_copy(out=t[:, lo:GP], in_=nm_ps[q][:, lo:GP])
-            nm_bc[q] = t
+        def spread_noise(g):
+            nb = psn.tile([P, GP // 2], F32, name="nb")
+            for jj in range(2):
+                nc.tensor.transpose(
+                    nb[:, P * jj : P * (jj + 1)],
+                    nm_pix[:, jj, g : g + 1].to_broadcast([P, P]),
+                    ident_f[:],
+                )
+            nm_ps[g] = nb
 
         n_sb = {}
         y_sb = {}
 
-        def noise_0(h, engine):
+        def noise(g, h, on_vector=False):
             if h == 0:
-                n_sb[0] = npool.tile([P, 2 * GP], F32, name="n_sb")
-            dst = n_sb[0][:, GP * h : GP * (h + 1)].rearrange("c (jj e p) -> c jj e p", jj=2, e=2)
-            src = nm_ps[0][:].bitcast(BF16)[:, 0:GP].rearrange("c (jj p e) -> c jj e p", jj=2, e=2)
+                n_sb[g] = npool.tile([P, 2 * GP], F32, name="n_sb")
+            dst = n_sb[g][:, GP * h : GP * (h + 1)].rearrange("c (jj e p) -> c jj e p", jj=2, e=2)
+            src = nm_ps[g][:].bitcast(BF16).rearrange("c (jj p e) -> c jj e p", jj=2, e=2)
             w_col, b_col = vec3[:, h, 0:1], vec3[:, 2 + h, 0:1]
-            if engine == "vector":
+            if on_vector:
                 nc.vector.tensor_scalar(
                     out=dst, in0=src, scalar1=w_col, scalar2=b_col, op0=ALU.mult, op1=ALU.add
                 )
             else:
-                nc.scalar.activation(
-                    out=dst, in_=src, func=ACT.Identity, scale=w_col, bias=b_col
-                )
-
-        def noise(g):
-            t = npool.tile([P, 2 * GP], F32, name="n_sb")
-            src = nm_bc[g // 2][:].bitcast(BF16)[:, GP * (g % 2) : GP * (g % 2 + 1)].rearrange(
-                "c (jj p e) -> c jj e p", jj=2, e=2
-            )
-            for h in range(2):
-                nc.gpsimd.tensor_scalar(
-                    out=t[:, GP * h : GP * (h + 1)].rearrange("c (jj e p) -> c jj e p", jj=2, e=2),
-                    in0=src,
-                    scalar1=vec3[:, h, 0:1],
-                    scalar2=vec3[:, 2 + h, 0:1],
-                    op0=ALU.mult,
-                    op1=ALU.add,
-                )
-            n_sb[g] = t
+                nc.scalar.activation(out=dst, in_=src, func=ACT.Identity, scale=w_col, bias=b_col)
 
         g1 = const.tile([P, 2 * P], F32, name="g1")
         bt = const.tile([P, 2 * P], F32, name="bt")
@@ -253,31 +228,29 @@ def tile_styleganlayerepilogue_t_kernel(
             nc.vector.quantize_mx(out=cd[:].bitcast(FP8X4), scales=sc[:], in_=grp[g][:])
             codes[g] = (cd, sc)
 
-        def products(g):
+        def products(g, h):
             cd, sc = codes[g]
-            for h in range(2):
-                acc = psp.tile([P, GP], F32, name="acc")
-                nc.tensor.matmul_mx(
-                    out=acc[:],
-                    lhsT=w_codes[:, P * h : P * (h + 1)].bitcast(FP8X4),
-                    lhsT_scale=w_scl[:, P * h : P * (h + 1)],
-                    rhs=cd[:].bitcast(FP8X4),
-                    rhs_scale=sc[:],
-                    start=True,
-                    stop=True,
-                )
-                prod[g, h] = acc
+            acc = psp.tile([P, GP], F32, name="acc")
+            nc.tensor.matmul_mx(
+                out=acc[:],
+                lhsT=w_codes[:, P * h : P * (h + 1)].bitcast(FP8X4),
+                lhsT_scale=w_scl[:, P * h : P * (h + 1)],
+                rhs=cd[:].bitcast(FP8X4),
+                rhs_scale=sc[:],
+                start=True,
+                stop=True,
+            )
+            prod[g, h] = acc
 
-        def add_noise(g):
-            t = ypool.tile([P, 2 * GP], F32, name="y_sb")
-            for h in range(2):
-                nc.vector.tensor_tensor(
-                    out=t[:, GP * h : GP * (h + 1)],
-                    in0=prod[g, h][:],
-                    in1=n_sb[g][:, GP * h : GP * (h + 1)],
-                    op=ALU.add,
-                )
-            y_sb[g] = t
+        def add_noise(g, h):
+            if h == 0:
+                y_sb[g] = ypool.tile([P, 2 * GP], F32, name="y_sb")
+            nc.vector.tensor_tensor(
+                out=y_sb[g][:, GP * h : GP * (h + 1)],
+                in0=prod[g, h][:],
+                in1=n_sb[g][:, GP * h : GP * (h + 1)],
+                op=ALU.add,
+            )
 
         def lrelu(g):
             for h in range(2):
@@ -310,8 +283,7 @@ def tile_styleganlayerepilogue_t_kernel(
                 bias=eps_t[:],
             )
 
-        def coefficients(g, eng, lo=0, hi=16):
-            st3 = stats[g][:].rearrange("c (n k) -> c n k", k=3)
+        def coefficient(g, step, lo=0, hi=16):
             if g not in coef:
                 a_t = spool.tile([P, 16], F32, name="a_t")
                 b_t = spool.tile([P, 16], F32, name="b_t")
@@ -319,31 +291,35 @@ def tile_styleganlayerepilogue_t_kernel(
                 coef[g] = (a_t, b_t, ma)
             a_t, b_t, ma = coef[g]
             cols = slice(16 * g + lo, 16 * g + hi)
-            eng.tensor_tensor(out=a_t[:, lo:hi], in0=rstd[g][:, lo:hi], in1=g1[:, cols], op=ALU.mult)
-            eng.tensor_tensor(out=ma[:, lo:hi], in0=st3[:, lo:hi, 1], in1=a_t[:, lo:hi], op=ALU.mult)
-            eng.tensor_tensor(out=b_t[:, lo:hi], in0=bt[:, cols], in1=ma[:, lo:hi], op=ALU.subtract)
+            mean = stats[g][:].rearrange("c (n k) -> c n k", k=3)[:, lo:hi, 1]
+            out_t, in0, in1, op = (
+                (a_t, rstd[g][:, lo:hi], g1[:, cols], ALU.mult),
+                (ma, mean, a_t[:, lo:hi], ALU.mult),
+                (b_t, bt[:, cols], ma[:, lo:hi], ALU.subtract),
+            )[step]
+            nc.vector.tensor_tensor(out=out_t[:, lo:hi], in0=in0, in1=in1, op=op)
 
-        def affine(g, h, on_vector):
+        def affine(g, lo, hi, on_vector):
             a_t, b_t, ma = coef[g]
-            yv = y_sb[g][:, GP * h : GP * (h + 1)].rearrange("c (j s q) -> c s j q", j=4, s=8, q=16)
-            for s in range(8):
-                lc = 8 * h + s
+            yv = y_sb[g][:].rearrange("c (h j s q) -> c h s j q", h=2, j=4, s=8, q=16)
+            for n in range(lo, hi):
+                yn = yv[:, n // 8, n % 8]
                 if on_vector:
                     nc.vector.tensor_scalar(
-                        out=yv[:, s],
-                        in0=yv[:, s],
-                        scalar1=a_t[:, lc : lc + 1],
-                        scalar2=b_t[:, lc : lc + 1],
+                        out=yn,
+                        in0=yn,
+                        scalar1=a_t[:, n : n + 1],
+                        scalar2=b_t[:, n : n + 1],
                         op0=ALU.mult,
                         op1=ALU.add,
                     )
                 else:
                     nc.scalar.activation(
-                        out=yv[:, s],
-                        in_=yv[:, s],
+                        out=yn,
+                        in_=yn,
                         func=ACT.Identity,
-                        scale=a_t[:, lc : lc + 1],
-                        bias=b_t[:, lc : lc + 1],
+                        scale=a_t[:, n : n + 1],
+                        bias=b_t[:, n : n + 1],
                     )
 
         def t_back(g, h):
@@ -382,72 +358,84 @@ def tile_styleganlayerepilogue_t_kernel(
         quant_w()
         vectors()
         quant(0)
-        spread_noise(0, psn, "nb")
-        noise_0(0, "vector")
-        noise_0(1, "scalar")
+        spread_noise(0)
+        noise(0, 0, True)
+        noise(0, 1)
         t_in(1, (0,))
-        products(0)
+        products(0, 0)
+        products(0, 1)
         t_in(1, (1,))
         x_out(1)
+        spread_noise(1)
         t_in(2)
-        add_noise(0)
-        keep_noise(0, nc.vector.tensor_copy, GP // 2)
+        noise(1, 0)
+        noise(1, 1)
         nc.vector.tensor_scalar_add(out=one_g[:], in0=vec3[:, 0:2, 1], scalar1=1.0)
-        noise(1)
         for i in range(NG):
-            if i + 1 < NG:
+            if i + 1 < NG and i > 0:
                 quant(i + 1)
-                products(i + 1)
-            if i >= 3 and i < NG - 1:
+            if i >= 3:
                 copy_out(i - 3, 0, nc.scalar.copy)
                 copy_out(i - 3, 1, nc.scalar.copy)
                 store(i - 3)
             if i + 2 < NG:
                 x_out(i + 2)
-            if i >= 1:
-                add_noise(i)
+            if i >= 2:
+                coefficient(i - 2, 0)
+            add_noise(i, 0)
+            if i >= 2:
+                coefficient(i - 2, 1)
+            add_noise(i, 1)
+            if i >= 2:
+                coefficient(i - 2, 2)
+            if i == 0:
+                quant(1)
+            if i + 1 < NG:
+                products(i + 1, 0)
+                products(i + 1, 1)
+            if i + 2 < NG:
+                spread_noise(i + 2)
             if i + 3 < NG:
                 t_in(i + 3)
-            if i < 3:
-                for q in range(3 * i + 1, min(3 * i + 4, NG // 2)):
-                    spread_noise(q, *((psn, "nb") if q % 2 else (pso, "ot")))
-                    keep_noise(q, nc.scalar.copy)
-            if i + 2 < NG:
-                noise(i + 2)
             if i >= 2:
-                affine(i - 2, 0, False)
+                affine(i - 2, 0, 8, False)
                 t_back(i - 2, 0)
-                affine(i - 2, 1, False)
-                t_back(i - 2, 1)
+                affine(i - 2, 8, N_SCALAR, False)
+            if i + 2 < NG:
+                noise(i + 2, 0)
+                noise(i + 2, 1)
             if i >= 1:
                 moments(i - 1)
+            if i >= 2:
+                affine(i - 2, N_SCALAR, 16, True)
+                t_back(i - 2, 1)
             if i == 0:
                 style_transposes()
             if i == 1:
                 style_copy()
                 style_matmuls()
             lrelu(i)
-            if i >= NG - 2:
-                copy_out(i - 2, 0, nc.scalar.copy)
-                copy_out(i - 2, 1, nc.scalar.copy)
-                store(i - 2)
             if i >= 1:
                 inv_std(i - 1)
-                coefficients(i - 1, nc.gpsimd)
-        g, z = NG - 2, NG - 1
+        f, g, z = NG - 3, NG - 2, NG - 1
+        copy_out(f, 0, nc.scalar.copy)
+        for step in range(3):
+            coefficient(g, step)
         moments(z, (0,))
-        affine(g, 0, False)
+        affine(g, 0, 8, False)
         t_back(g, 0)
+        copy_out(f, 1, nc.scalar.copy)
+        store(f)
         inv_std(z, 0, 8)
-        coefficients(z, nc.gpsimd, 0, 8)
         moments(z, (1,))
-        affine(g, 1, True)
-        t_back(g, 1)
         inv_std(z, 8, 16)
+        affine(g, 8, 16, True)
+        t_back(g, 1)
+        for step in range(3):
+            coefficient(z, step)
         copy_out(g, 0, nc.scalar.copy)
-        coefficients(z, nc.vector, 8, 16)
-        affine(z, 0, False)
-        affine(z, 1, True)
+        affine(z, 0, 8, False)
+        affine(z, 8, 16, True)
         copy_out(g, 1, nc.scalar.copy)
         store(g)
         t_back(z, 0)

@@ -38,12 +38,14 @@ def tile_styleganlayerepilogue_t_kernel(
         npool = ctx.enter_context(tc.tile_pool(name="npool", bufs=2))
         ypool = ctx.enter_context(tc.tile_pool(name="ypool", bufs=4))
         gpool = ctx.enter_context(tc.tile_pool(name="gpool", bufs=3))
-        spool = ctx.enter_context(tc.tile_pool(name="spool", bufs=5))
+        spool = ctx.enter_context(tc.tile_pool(name="spool", bufs=4))
         opool = ctx.enter_context(tc.tile_pool(name="opool", bufs=3))
         psx = ctx.enter_context(tc.psum_pool(name="psx", bufs=2))
         psp = ctx.enter_context(tc.psum_pool(name="psp", bufs=3))
         psn = ctx.enter_context(tc.psum_pool(name="psn", bufs=1))
         pso = ctx.enter_context(tc.psum_pool(name="pso", bufs=2))
+
+        half = GP // 2
 
         ident_f = const.tile([P, P], F32, name="ident_f")
         make_identity(nc, ident_f[:])
@@ -61,25 +63,28 @@ def tile_styleganlayerepilogue_t_kernel(
         def load_x(g):
             t = xpool.tile([P, 4 * CIN], BF16, name="x_sb")
             nc.sync.dma_start(
-                out=t[:],
-                in_=x_rows[GP * g : GP * (g + 1), :].rearrange("(p j) k -> p (j k)", j=4),
+                out=t[:].rearrange("p (j k) -> p j k", j=4),
+                in_=x_rows[GP * g : GP * (g + 1), :].rearrange("(j p) k -> p j k", j=4),
             )
             x_sb.append(t)
 
         x_0 = xpool.tile([P, 4 * CIN], BF16, name="x_sb")
-        x_rows_0 = x_rows[0:GP, :].rearrange("(p j) k -> p (j k)", j=4)
-        for jj in range(2):
-            cols = slice(2 * CIN * jj, 2 * CIN * (jj + 1))
-            nc.sync.dma_start(out=x_0[:, cols], in_=x_rows_0[:, cols])
         x_sb.append(x_0)
+
+        def load_x0(jj):
+            nc.sync.dma_start(
+                out=x_0[:, 2 * CIN * jj : 2 * CIN * (jj + 1)].rearrange("p (j k) -> p j k", j=2),
+                in_=x_rows[half * jj : half * (jj + 1), :].rearrange("(j p) k -> p j k", j=2),
+            )
+
+        load_x0(0)
         nc.sync.dma_start(out=rows[0:NG, :], in_=nm_flat.rearrange("(g n) -> g n", n=GP))
         nc.sync.dma_start(out=rows[16:17, 0:NF], in_=noise_weight.rearrange("a b c n -> (a b c) n"))
         nc.sync.dma_start(out=rows[16:17, NF : 2 * NF], in_=bias.rearrange("a b c n -> (a b c) n"))
         nc.sync.dma_start(out=rows[17:18, :], in_=dense_b.rearrange("(o n) -> o n", o=1))
         w_raw = const.tile([P, 4 * NF], BF16, name="w_raw")
         nc.sync.dma_start(out=w_raw[:], in_=conv_w.rearrange("(i t) c -> i (t c)", t=4))
-        load_x(1)
-        load_x(2)
+        load_x0(1)
         dl_sb = const.tile([P, 512], BF16, name="dl_sb")
         nc.sync.dma_start(out=dl_sb[:], in_=dlatents)
         dw_sb = const.tile([P, 2048], BF16, name="dw_sb")
@@ -87,7 +92,7 @@ def tile_styleganlayerepilogue_t_kernel(
             out=dw_sb[:].rearrange("p (kb n) -> p kb n", kb=4),
             in_=dense_w.rearrange("(kb p) n -> p kb n", p=P),
         )
-        for g in range(3, NG):
+        for g in range(1, NG):
             load_x(g)
 
         w_grp = const.tile([P, 4 * NF], BF16, name="w_grp", align_bytes=64)
@@ -111,10 +116,10 @@ def tile_styleganlayerepilogue_t_kernel(
             vps = pso.tile([P, 4, P], BF16, name="vps", tag="ot")
             rows_32 = rows[:].bitcast(F32)
             for jj in range(2):
-                nc.tensor.transpose(nps[:, jj, :], rows_32[:, jj : GP // 2 : 2], ident_f[:])
+                nc.tensor.transpose(nps[:, jj, :], rows_32[:, P * jj : P * (jj + 1)], ident_f[:])
             for b in range(4):
                 nc.tensor.transpose(vps[:, b, :], rows[:, P * b : P * (b + 1)], ident_b[:])
-            nc.scalar.copy(out=nm_pix[:], in_=nps[:, :, 0:NG])
+            nc.vector.tensor_copy(out=nm_pix[:], in_=nps[:, :, 0:NG])
             nc.vector.tensor_copy(out=vec3, in_=vps[:, :, 16:18])
 
         nm_ps = {}
@@ -135,15 +140,14 @@ def tile_styleganlayerepilogue_t_kernel(
         def noise(g, h, on_vector=False):
             if h == 0:
                 n_sb[g] = npool.tile([P, 2 * GP], F32, name="n_sb")
-            dst = n_sb[g][:, GP * h : GP * (h + 1)].rearrange("c (jj e p) -> c jj e p", jj=2, e=2)
-            src = nm_ps[g][:].bitcast(BF16).rearrange("c (jj p e) -> c jj e p", jj=2, e=2)
-            w_col, b_col = vec3[:, h, 0:1], vec3[:, 2 + h, 0:1]
-            if on_vector:
-                nc.vector.tensor_scalar(
-                    out=dst, in0=src, scalar1=w_col, scalar2=b_col, op0=ALU.mult, op1=ALU.add
-                )
-            else:
-                nc.scalar.activation(out=dst, in_=src, func=ACT.Identity, scale=w_col, bias=b_col)
+            dst = n_sb[g][:, GP * h : GP * (h + 1)]
+            nc.scalar.activation(
+                out=dst,
+                in_=nm_ps[g][:].bitcast(BF16),
+                func=ACT.Identity,
+                scale=vec3[:, h, 0:1],
+                bias=vec3[:, 2 + h, 0:1],
+            )
 
         g1 = const.tile([P, 2 * P], F32, name="g1")
         bt = const.tile([P, 2 * P], F32, name="bt")
@@ -172,6 +176,10 @@ def tile_styleganlayerepilogue_t_kernel(
                         start=(kb == 0),
                         stop=(kb == 3),
                     )
+            style_ps["gb"] = gb
+
+        def style_scales():
+            gb = style_ps["gb"]
             g1v = g1[:].rearrange("c (g h s) -> c h g s", h=2, s=8)
             btv = bt[:].rearrange("c (g h s) -> c h g s", h=2, s=8)
             for h in range(2):
@@ -212,52 +220,53 @@ def tile_styleganlayerepilogue_t_kernel(
                         )
                 xts[g, jj] = xt
 
-        def x_out(g):
-            t = gpool.tile([P, 4 * GP], BF16, name="grp", align_bytes=64)
-            t32 = t[:].bitcast(F32)
-            for jj in range(2):
+        def x_out(g, parts=(0, 1)):
+            if g not in grp:
+                grp[g] = gpool.tile([P, 4 * GP], BF16, name="grp", align_bytes=64)
+            t32 = grp[g][:].bitcast(F32)
+            for jj in parts:
                 nc.scalar.copy(
                     out=t32[:, 512 * jj : 512 * (jj + 1)].rearrange("p (c u) -> p c u", u=2),
                     in_=xts[g, jj][:].rearrange("p (u c) -> p c u", u=2),
                 )
-            grp[g] = t
 
-        def quant(g):
-            cd = gpool.tile([P, GP], U32, name="codes", align_bytes=64)
-            sc = gpool.tile([P, GP], U8, name="scl", align_bytes=64)
-            nc.vector.quantize_mx(out=cd[:].bitcast(FP8X4), scales=sc[:], in_=grp[g][:])
-            codes[g] = (cd, sc)
-
-        def products(g, h):
+        def quant(g, lo=0, hi=GP):
+            if g not in codes:
+                cd = gpool.tile([P, GP], U32, name="codes", align_bytes=64)
+                sc = gpool.tile([P, GP], U8, name="scl", align_bytes=64)
+                codes[g] = (cd, sc)
             cd, sc = codes[g]
-            acc = psp.tile([P, GP], F32, name="acc")
+            nc.vector.quantize_mx(
+                out=cd[:, lo:hi].bitcast(FP8X4), scales=sc[:, lo:hi], in_=grp[g][:, 4 * lo : 4 * hi]
+            )
+
+        def products(g, h, lo=0, hi=GP):
+            cd, sc = codes[g]
+            if (g, h) not in prod:
+                prod[g, h] = psp.tile([P, GP], F32, name="acc")
             nc.tensor.matmul_mx(
-                out=acc[:],
+                out=prod[g, h][:, lo:hi],
                 lhsT=w_codes[:, P * h : P * (h + 1)].bitcast(FP8X4),
                 lhsT_scale=w_scl[:, P * h : P * (h + 1)],
-                rhs=cd[:].bitcast(FP8X4),
-                rhs_scale=sc[:],
+                rhs=cd[:, lo:hi].bitcast(FP8X4),
+                rhs_scale=sc[:, lo:hi],
                 start=True,
                 stop=True,
             )
-            prod[g, h] = acc
 
-        def add_noise(g, h):
-            if h == 0:
+        def add_noise(g, h, lo=0, hi=GP):
+            if g not in y_sb:
                 y_sb[g] = ypool.tile([P, 2 * GP], F32, name="y_sb")
+            cols = slice(GP * h + lo, GP * h + hi)
             nc.vector.tensor_tensor(
-                out=y_sb[g][:, GP * h : GP * (h + 1)],
-                in0=prod[g, h][:],
-                in1=n_sb[g][:, GP * h : GP * (h + 1)],
-                op=ALU.add,
+                out=y_sb[g][:, cols], in0=prod[g, h][:, lo:hi], in1=n_sb[g][:, cols], op=ALU.add
             )
 
-        def lrelu(g):
-            for h in range(2):
-                th = y_sb[g][:, GP * h : GP * (h + 1)]
-                nc.vector.scalar_tensor_tensor(
-                    out=th, in0=th, scalar=SLOPE, in1=th, op0=ALU.mult, op1=ALU.max
-                )
+        def lrelu(g, h):
+            th = y_sb[g][:, GP * h : GP * (h + 1)]
+            nc.vector.scalar_tensor_tensor(
+                out=th, in0=th, scalar=SLOPE, in1=th, op0=ALU.mult, op1=ALU.max
+            )
 
         def moments(g, halves=(0, 1)):
             if g not in stats:
@@ -265,7 +274,7 @@ def tile_styleganlayerepilogue_t_kernel(
             st = stats[g]
             for h in halves:
                 yv = y_sb[g][:, GP * h : GP * (h + 1)].rearrange(
-                    "c (j sp s2 q) -> c sp j q s2", j=4, sp=4, s2=2, q=16
+                    "c (sp s2 q) -> c sp q s2", sp=4, s2=2, q=64
                 )
                 for sp in range(4):
                     idx = h * 4 + sp
@@ -301,7 +310,7 @@ def tile_styleganlayerepilogue_t_kernel(
 
         def affine(g, lo, hi, on_vector):
             a_t, b_t, ma = coef[g]
-            yv = y_sb[g][:].rearrange("c (h j s q) -> c h s j q", h=2, j=4, s=8, q=16)
+            yv = y_sb[g][:].rearrange("c (h s q) -> c h s q", h=2, s=8, q=64)
             for n in range(lo, hi):
                 yn = yv[:, n // 8, n % 8]
                 if on_vector:
@@ -343,103 +352,115 @@ def tile_styleganlayerepilogue_t_kernel(
 
         def store(g):
             nc.sync.dma_start(
-                out=out_rows[GP * g : GP * (g + 1), :].rearrange("(p j) c -> p (j c)", j=4),
-                in_=o_sb[g][:],
+                out=out_rows[GP * g : GP * (g + 1), :].rearrange("(j p) c -> p j c", j=4),
+                in_=o_sb[g][:].rearrange("p (j c) -> p j c", c=NF),
             )
 
         def store_half(g, h):
             ov = o_sb[g][:].rearrange("p (j c) -> p j c", c=NF)
-            dst = out_rows[GP * g : GP * (g + 1), :].rearrange("(p j) c -> p j c", j=4)
+            dst = out_rows[GP * g : GP * (g + 1), :].rearrange("(j p) c -> p j c", j=4)
             cols = slice(P * h, P * (h + 1))
             nc.sync.dma_start(out=dst[:, :, cols], in_=ov[:, :, cols])
 
-        t_in(0)
-        x_out(0)
-        quant_w()
+        t_in(0, (0,))
+        x_out(0, (0,))
         vectors()
-        quant(0)
+        quant_w()
         spread_noise(0)
-        noise(0, 0, True)
+        quant(0, 0, half)
+        t_in(0, (1,))
+        noise(0, 0)
+        products(0, 0, 0, half)
+        products(0, 1, 0, half)
+        x_out(0, (1,))
         noise(0, 1)
-        t_in(1, (0,))
-        products(0, 0)
-        products(0, 1)
-        t_in(1, (1,))
+        add_noise(0, 0, 0, half)
+        quant(0, half, GP)
+        products(0, 0, half, GP)
+        products(0, 1, half, GP)
+        t_in(1)
         x_out(1)
+        add_noise(0, 1, 0, half)
+        add_noise(0, 0, half, GP)
+        add_noise(0, 1, half, GP)
         spread_noise(1)
-        t_in(2)
+        style_transposes()
         noise(1, 0)
         noise(1, 1)
         nc.vector.tensor_scalar_add(out=one_g[:], in0=vec3[:, 0:2, 1], scalar1=1.0)
+        t_in(2)
         for i in range(NG):
-            if i + 1 < NG and i > 0:
-                quant(i + 1)
-            if i >= 3:
-                copy_out(i - 3, 0, nc.scalar.copy)
-                copy_out(i - 3, 1, nc.scalar.copy)
-                store(i - 3)
-            if i + 2 < NG:
-                x_out(i + 2)
-            if i >= 2:
-                coefficient(i - 2, 0)
-            add_noise(i, 0)
-            if i >= 2:
-                coefficient(i - 2, 1)
-            add_noise(i, 1)
-            if i >= 2:
-                coefficient(i - 2, 2)
+            if i >= 1:
+                inv_std(i - 1)
+                add_noise(i, 0)
+            if i == NG - 1:
+                coefficient(i - 1, 0)
+            if i >= 1:
+                add_noise(i, 1)
             if i == 0:
-                quant(1)
+                lrelu(0, 0)
+                lrelu(0, 1)
+                style_copy()
+            if i + 2 < NG:
+                spread_noise(i + 2)
+            if i >= 2:
+                t_back(i - 2, 0)
+                t_back(i - 2, 1)
             if i + 1 < NG:
+                quant(i + 1)
+                if i >= 2:
+                    coefficient(i - 1, 0)
                 products(i + 1, 0)
                 products(i + 1, 1)
             if i + 2 < NG:
-                spread_noise(i + 2)
+                x_out(i + 2)
+            if i >= 2:
+                copy_out(i - 2, 0, nc.scalar.copy)
+                copy_out(i - 2, 1, nc.scalar.copy)
+                store(i - 2)
             if i + 3 < NG:
                 t_in(i + 3)
-            if i >= 2:
-                affine(i - 2, 0, 8, False)
-                t_back(i - 2, 0)
-                affine(i - 2, 8, N_SCALAR, False)
+            if i == 0:
+                style_matmuls()
+            if i == 1:
+                style_scales()
             if i + 2 < NG:
                 noise(i + 2, 0)
                 noise(i + 2, 1)
             if i >= 1:
-                moments(i - 1)
+                lrelu(i, 0)
             if i >= 2:
-                affine(i - 2, N_SCALAR, 16, True)
-                t_back(i - 2, 1)
-            if i == 0:
-                style_transposes()
-            if i == 1:
-                style_copy()
-                style_matmuls()
-            lrelu(i)
+                coefficient(i - 1, 1)
             if i >= 1:
-                inv_std(i - 1)
-        f, g, z = NG - 3, NG - 2, NG - 1
-        copy_out(f, 0, nc.scalar.copy)
-        for step in range(3):
-            coefficient(g, step)
-        moments(z, (0,))
-        affine(g, 0, 8, False)
+                lrelu(i, 1)
+            if i >= 2:
+                coefficient(i - 1, 2)
+            if i == 1:
+                for step in range(3):
+                    coefficient(0, step)
+            if i >= 1:
+                affine(i - 1, 0, N_SCALAR, False)
+            moments(i, (0,))
+            if i == NG - 1:
+                inv_std(i, 0, 8)
+            if i >= 1:
+                affine(i - 1, N_SCALAR, 16, True)
+            moments(i, (1,))
+        g, z = NG - 2, NG - 1
         t_back(g, 0)
-        copy_out(f, 1, nc.scalar.copy)
-        store(f)
-        inv_std(z, 0, 8)
-        moments(z, (1,))
-        inv_std(z, 8, 16)
-        affine(g, 8, 16, True)
         t_back(g, 1)
-        for step in range(3):
-            coefficient(z, step)
         copy_out(g, 0, nc.scalar.copy)
+        inv_std(z, 8, 16)
+        for step in range(3):
+            coefficient(z, step, 0, 8)
         affine(z, 0, 8, False)
+        t_back(z, 0)
+        for step in range(3):
+            coefficient(z, step, 8, 16)
         affine(z, 8, 16, True)
+        t_back(z, 1)
         copy_out(g, 1, nc.scalar.copy)
         store(g)
-        t_back(z, 0)
-        t_back(z, 1)
         copy_out(z, 0, nc.scalar.copy)
         copy_out(z, 1, nc.vector.tensor_copy)
         store_half(z, 0)

@@ -19,7 +19,7 @@ GP = 512
 NG = PIX // GP
 EPS = 1e-8
 SLOPE = 0.2
-N_SCALAR = 12
+N_SCALAR = 16
 FLOPS = 2 * PIX * CIN * NF + 2 * 128 * 512 * 512
 
 
@@ -35,7 +35,7 @@ def tile_styleganlayerepilogue_t_kernel(
         ctx.enter_context(tc.manual_schedule())
         const = ctx.enter_context(tc.tile_pool(name="const", bufs=1))
         xpool = ctx.enter_context(tc.tile_pool(name="xpool", bufs=NG))
-        npool = ctx.enter_context(tc.tile_pool(name="npool", bufs=2))
+        zpool = ctx.enter_context(tc.tile_pool(name="zpool", bufs=2))
         ypool = ctx.enter_context(tc.tile_pool(name="ypool", bufs=4))
         gpool = ctx.enter_context(tc.tile_pool(name="gpool", bufs=3))
         spool = ctx.enter_context(tc.tile_pool(name="spool", bufs=4))
@@ -123,31 +123,51 @@ def tile_styleganlayerepilogue_t_kernel(
             nc.vector.tensor_copy(out=vec3, in_=vps[:, :, 16:18])
 
         nm_ps = {}
+        nm_bc = {}
 
-        def spread_noise(g):
-            nb = psn.tile([P, GP // 2], F32, name="nb")
-            for jj in range(2):
-                nc.tensor.transpose(
-                    nb[:, P * jj : P * (jj + 1)],
-                    nm_pix[:, jj, g : g + 1].to_broadcast([P, P]),
-                    ident_f[:],
-                )
-            nm_ps[g] = nb
+        def spread_noise(q):
+            nb = (pso if q == 1 else psn).tile([P, GP], F32, name="nb", tag="ot" if q == 1 else "nb")
+            for e in range(2):
+                for jj in range(2):
+                    lo = half * e + P * jj
+                    nc.tensor.transpose(
+                        nb[:, lo : lo + P],
+                        nm_pix[:, jj, 2 * q + e : 2 * q + e + 1].to_broadcast([P, P]),
+                        ident_f[:],
+                    )
+            nm_ps[q] = nb
 
-        n_sb = {}
+        def keep_noise(q):
+            t = const.tile([P, GP], F32, name="nm_bc%d" % q)
+            nc.scalar.copy(out=t[:], in_=nm_ps[q][:])
+            nm_bc[q] = t
+
+        z_sb = {}
         y_sb = {}
 
-        def noise(g, h, on_vector=False):
-            if h == 0:
-                n_sb[g] = npool.tile([P, 2 * GP], F32, name="n_sb")
-            dst = n_sb[g][:, GP * h : GP * (h + 1)]
-            nc.scalar.activation(
-                out=dst,
-                in_=nm_ps[g][:].bitcast(BF16),
-                func=ACT.Identity,
-                scale=vec3[:, h, 0:1],
-                bias=vec3[:, 2 + h, 0:1],
-            )
+        def noise(g, h, on_scalar=False):
+            if g not in z_sb:
+                z_sb[g] = zpool.tile([P, 2 * GP], F32, name="z_sb")
+            dst = z_sb[g][:, GP * h : GP * (h + 1)]
+            cols = slice(GP * (g % 2), GP * (g % 2 + 1))
+            w_col, b_col = vec3[:, h, 0:1], vec3[:, 2 + h, 0:1]
+            if on_scalar:
+                nc.scalar.activation(
+                    out=dst,
+                    in_=nm_ps[g // 2][:].bitcast(BF16)[:, cols],
+                    func=ACT.Identity,
+                    scale=w_col,
+                    bias=b_col,
+                )
+            else:
+                nc.gpsimd.tensor_scalar(
+                    out=dst,
+                    in0=nm_bc[g // 2][:].bitcast(BF16)[:, cols],
+                    scalar1=w_col,
+                    scalar2=b_col,
+                    op0=ALU.mult,
+                    op1=ALU.add,
+                )
 
         g1 = const.tile([P, 2 * P], F32, name="g1")
         bt = const.tile([P, 2 * P], F32, name="bt")
@@ -255,17 +275,16 @@ def tile_styleganlayerepilogue_t_kernel(
             )
 
         def add_noise(g, h, lo=0, hi=GP):
+            zc = z_sb[g][:, GP * h + lo : GP * h + hi]
+            nc.vector.tensor_tensor(out=zc, in0=prod[g, h][:, lo:hi], in1=zc, op=ALU.add)
+
+        def lrelu(g, lo, hi):
             if g not in y_sb:
                 y_sb[g] = ypool.tile([P, 2 * GP], F32, name="y_sb")
-            cols = slice(GP * h + lo, GP * h + hi)
-            nc.vector.tensor_tensor(
-                out=y_sb[g][:, cols], in0=prod[g, h][:, lo:hi], in1=n_sb[g][:, cols], op=ALU.add
-            )
-
-        def lrelu(g, h):
-            th = y_sb[g][:, GP * h : GP * (h + 1)]
+            cols = slice(lo, hi)
+            zh = z_sb[g][:, cols]
             nc.vector.scalar_tensor_tensor(
-                out=th, in0=th, scalar=SLOPE, in1=th, op0=ALU.mult, op1=ALU.max
+                out=y_sb[g][:, cols], in0=zh, scalar=SLOPE, in1=zh, op0=ALU.mult, op1=ALU.max
             )
 
         def moments(g, halves=(0, 1)):
@@ -369,11 +388,11 @@ def tile_styleganlayerepilogue_t_kernel(
         spread_noise(0)
         quant(0, 0, half)
         t_in(0, (1,))
-        noise(0, 0)
+        noise(0, 0, True)
         products(0, 0, 0, half)
         products(0, 1, 0, half)
         x_out(0, (1,))
-        noise(0, 1)
+        noise(0, 1, True)
         add_noise(0, 0, 0, half)
         quant(0, half, GP)
         products(0, 0, half, GP)
@@ -383,10 +402,10 @@ def tile_styleganlayerepilogue_t_kernel(
         add_noise(0, 1, 0, half)
         add_noise(0, 0, half, GP)
         add_noise(0, 1, half, GP)
+        noise(1, 0, True)
+        noise(1, 1, True)
         spread_noise(1)
         style_transposes()
-        noise(1, 0)
-        noise(1, 1)
         nc.vector.tensor_scalar_add(out=one_g[:], in0=vec3[:, 0:2, 1], scalar1=1.0)
         t_in(2)
         for i in range(NG):
@@ -398,11 +417,12 @@ def tile_styleganlayerepilogue_t_kernel(
             if i >= 1:
                 add_noise(i, 1)
             if i == 0:
-                lrelu(0, 0)
-                lrelu(0, 1)
-                style_copy()
-            if i + 2 < NG:
-                spread_noise(i + 2)
+                lrelu(0, 0, GP)
+                lrelu(0, GP, 2 * GP)
+            if i % 2 == 0 and i // 2 + 1 < NG // 2:
+                keep_noise(i // 2 + 1)
+            if i % 2 == 1 and i // 2 + 2 < NG // 2:
+                spread_noise(i // 2 + 2)
             if i >= 2:
                 t_back(i - 2, 0)
                 t_back(i - 2, 1)
@@ -412,6 +432,8 @@ def tile_styleganlayerepilogue_t_kernel(
                     coefficient(i - 1, 0)
                 products(i + 1, 0)
                 products(i + 1, 1)
+            if i == 0:
+                style_copy()
             if i + 2 < NG:
                 x_out(i + 2)
             if i >= 2:
@@ -424,28 +446,31 @@ def tile_styleganlayerepilogue_t_kernel(
                 style_matmuls()
             if i == 1:
                 style_scales()
-            if i + 2 < NG:
-                noise(i + 2, 0)
-                noise(i + 2, 1)
             if i >= 1:
-                lrelu(i, 0)
+                lrelu(i, 0, GP)
             if i >= 2:
                 coefficient(i - 1, 1)
             if i >= 1:
-                lrelu(i, 1)
+                lrelu(i, GP, GP + half)
             if i >= 2:
                 coefficient(i - 1, 2)
-            if i == 1:
-                for step in range(3):
-                    coefficient(0, step)
             if i >= 1:
+                lrelu(i, GP + half, 2 * GP)
+            if i + 2 < NG:
+                noise(i + 2, 1)
+                noise(i + 2, 0)
+            if i >= 2:
                 affine(i - 1, 0, N_SCALAR, False)
             moments(i, (0,))
             if i == NG - 1:
                 inv_std(i, 0, 8)
-            if i >= 1:
+            if i >= 2:
                 affine(i - 1, N_SCALAR, 16, True)
             moments(i, (1,))
+            if i == 1:
+                for step in range(3):
+                    coefficient(0, step)
+                affine(0, 0, 16, False)
         g, z = NG - 2, NG - 1
         t_back(g, 0)
         t_back(g, 1)

@@ -19,7 +19,6 @@ GP = 512
 NG = PIX // GP
 EPS = 1e-8
 SLOPE = 0.2
-N_SCALAR = 16
 FLOPS = 2 * PIX * CIN * NF + 2 * 128 * 512 * 512
 
 
@@ -311,7 +310,7 @@ def tile_styleganlayerepilogue_t_kernel(
                 bias=eps_t[:],
             )
 
-        def coefficient(g, step, lo=0, hi=16):
+        def coefficient(g, step, lo=0, hi=16, eng=nc.vector):
             if g not in coef:
                 a_t = spool.tile([P, 16], F32, name="a_t")
                 b_t = spool.tile([P, 16], F32, name="b_t")
@@ -325,7 +324,7 @@ def tile_styleganlayerepilogue_t_kernel(
                 (ma, mean, a_t[:, lo:hi], ALU.mult),
                 (b_t, bt[:, cols], ma[:, lo:hi], ALU.subtract),
             )[step]
-            nc.vector.tensor_tensor(out=out_t[:, lo:hi], in0=in0, in1=in1, op=op)
+            eng.tensor_tensor(out=out_t[:, lo:hi], in0=in0, in1=in1, op=op)
 
         def affine(g, lo, hi, on_vector):
             a_t, b_t, ma = coef[g]
@@ -375,12 +374,6 @@ def tile_styleganlayerepilogue_t_kernel(
                 in_=o_sb[g][:].rearrange("p (j c) -> p j c", c=NF),
             )
 
-        def store_half(g, h):
-            ov = o_sb[g][:].rearrange("p (j c) -> p j c", c=NF)
-            dst = out_rows[GP * g : GP * (g + 1), :].rearrange("(j p) c -> p j c", j=4)
-            cols = slice(P * h, P * (h + 1))
-            nc.sync.dma_start(out=dst[:, :, cols], in_=ov[:, :, cols])
-
         t_in(0, (0,))
         x_out(0, (0,))
         vectors()
@@ -412,10 +405,11 @@ def tile_styleganlayerepilogue_t_kernel(
             if i >= 1:
                 inv_std(i - 1)
                 add_noise(i, 0)
-            if i == NG - 1:
-                coefficient(i - 1, 0)
             if i >= 1:
                 add_noise(i, 1)
+            if i >= 2:
+                for step in range(3):
+                    coefficient(i - 1, step, eng=nc.gpsimd)
             if i == 0:
                 lrelu(0, 0, GP)
                 lrelu(0, GP, 2 * GP)
@@ -428,8 +422,6 @@ def tile_styleganlayerepilogue_t_kernel(
                 t_back(i - 2, 1)
             if i + 1 < NG:
                 quant(i + 1)
-                if i >= 2:
-                    coefficient(i - 1, 0)
                 products(i + 1, 0)
                 products(i + 1, 1)
             if i == 0:
@@ -448,24 +440,14 @@ def tile_styleganlayerepilogue_t_kernel(
                 style_scales()
             if i >= 1:
                 lrelu(i, 0, GP)
-            if i >= 2:
-                coefficient(i - 1, 1)
             if i >= 1:
-                lrelu(i, GP, GP + half)
-            if i >= 2:
-                coefficient(i - 1, 2)
-            if i >= 1:
-                lrelu(i, GP + half, 2 * GP)
+                lrelu(i, GP, 2 * GP)
             if i + 2 < NG:
                 noise(i + 2, 1)
                 noise(i + 2, 0)
             if i >= 2:
-                affine(i - 1, 0, N_SCALAR, False)
+                affine(i - 1, 0, 16 if i < NG - 1 else 8, False)
             moments(i, (0,))
-            if i == NG - 1:
-                inv_std(i, 0, 8)
-            if i >= 2:
-                affine(i - 1, N_SCALAR, 16, True)
             moments(i, (1,))
             if i == 1:
                 for step in range(3):
@@ -473,20 +455,18 @@ def tile_styleganlayerepilogue_t_kernel(
                 affine(0, 0, 16, False)
         g, z = NG - 2, NG - 1
         t_back(g, 0)
+        affine(g, 8, 16, True)
         t_back(g, 1)
+        inv_std(z)
+        for step in range(3):
+            coefficient(z, step)
         copy_out(g, 0, nc.scalar.copy)
-        inv_std(z, 8, 16)
-        for step in range(3):
-            coefficient(z, step, 0, 8)
-        affine(z, 0, 8, False)
-        t_back(z, 0)
-        for step in range(3):
-            coefficient(z, step, 8, 16)
         affine(z, 8, 16, True)
+        affine(z, 0, 8, False)
         t_back(z, 1)
-        copy_out(g, 1, nc.scalar.copy)
+        t_back(z, 0)
+        copy_out(g, 1, nc.vector.tensor_copy)
         store(g)
         copy_out(z, 0, nc.scalar.copy)
         copy_out(z, 1, nc.vector.tensor_copy)
-        store_half(z, 0)
-        store_half(z, 1)
+        store(z)

@@ -286,57 +286,55 @@ def tile_styleganlayerepilogue_t_kernel(
                 out=y_sb[g][:, cols], in0=zh, scalar=SLOPE, in1=zh, op0=ALU.mult, op1=ALU.max
             )
 
-        def moments(g, halves=(0, 1)):
-            if g not in stats:
-                stats[g] = spool.tile([P, 48], F32, name="st")
-            st = stats[g]
-            for h in halves:
-                yv = y_sb[g][:, GP * h : GP * (h + 1)].rearrange(
-                    "c (sp s2 q) -> c sp q s2", sp=4, s2=2, q=64
-                )
-                for sp in range(4):
-                    idx = h * 4 + sp
-                    nc.vector.bn_stats(out=st[:, 6 * idx : 6 * idx + 6], in_=yv[:, sp])
+        def moments(g):
+            if g // 2 not in stats:
+                stats[g // 2] = spool.tile([P, 96], F32, name="st")
+            st = stats[g // 2]
+            yv = y_sb[g][:].rearrange("c (sp s2 q) -> c sp q s2", s2=2, q=64)
+            for sp in range(8):
+                lo = 48 * (g % 2) + 6 * sp
+                nc.vector.bn_stats(out=st[:, lo : lo + 6], in_=yv[:, sp])
 
-        def inv_std(g, lo=0, hi=16):
-            st3 = stats[g][:].rearrange("c (n k) -> c n k", k=3)
-            if g not in rstd:
-                rstd[g] = spool.tile([P, 16], F32, name="rs")
+        def inv_std(g):
+            st3 = stats[g // 2][:].rearrange("c (n k) -> c n k", k=3)
+            if g // 2 not in rstd:
+                rstd[g // 2] = spool.tile([P, 32], F32, name="rs")
+            cols = slice(16 * (g % 2), 16 * (g % 2 + 1))
             nc.scalar.activation(
-                out=rstd[g][:, lo:hi],
-                in_=st3[:, lo:hi, 2],
+                out=rstd[g // 2][:, cols],
+                in_=st3[:, cols, 2],
                 func=ACT.Abs_reciprocal_sqrt,
                 scale=1.0 / 64.0,
                 bias=eps_t[:],
             )
 
-        def coefficient(g, step, lo=0, hi=16, eng=nc.vector):
-            if g not in coef:
-                a_t = spool.tile([P, 16], F32, name="a_t")
-                b_t = spool.tile([P, 16], F32, name="b_t")
-                ma = spool.tile([P, 16], F32, name="ma")
-                coef[g] = (a_t, b_t, ma)
-            a_t, b_t, ma = coef[g]
-            cols = slice(16 * g + lo, 16 * g + hi)
-            mean = stats[g][:].rearrange("c (n k) -> c n k", k=3)[:, lo:hi, 1]
+        def coefficient(q, step, lo=0, hi=32):
+            if q not in coef:
+                a_t = spool.tile([P, 32], F32, name="a_t")
+                b_t = spool.tile([P, 32], F32, name="b_t")
+                ma = spool.tile([P, 32], F32, name="ma")
+                coef[q] = (a_t, b_t, ma)
+            a_t, b_t, ma = coef[q]
+            cols = slice(32 * q + lo, 32 * q + hi)
+            mean = stats[q][:].rearrange("c (n k) -> c n k", k=3)[:, lo:hi, 1]
             out_t, in0, in1, op = (
-                (a_t, rstd[g][:, lo:hi], g1[:, cols], ALU.mult),
+                (a_t, rstd[q][:, lo:hi], g1[:, cols], ALU.mult),
                 (ma, mean, a_t[:, lo:hi], ALU.mult),
                 (b_t, bt[:, cols], ma[:, lo:hi], ALU.subtract),
             )[step]
-            eng.tensor_tensor(out=out_t[:, lo:hi], in0=in0, in1=in1, op=op)
+            nc.vector.tensor_tensor(out=out_t[:, lo:hi], in0=in0, in1=in1, op=op)
 
         def affine(g, lo, hi, on_vector):
-            a_t, b_t, ma = coef[g]
-            yv = y_sb[g][:].rearrange("c (h s q) -> c h s q", h=2, s=8, q=64)
+            a_t, b_t, ma = coef[g // 2]
             for n in range(lo, hi):
-                yn = yv[:, n // 8, n % 8]
+                yn = y_sb[g][:, 64 * n : 64 * (n + 1)]
+                k = 16 * (g % 2) + n
                 if on_vector:
                     nc.vector.tensor_scalar(
                         out=yn,
                         in0=yn,
-                        scalar1=a_t[:, n : n + 1],
-                        scalar2=b_t[:, n : n + 1],
+                        scalar1=a_t[:, k : k + 1],
+                        scalar2=b_t[:, k : k + 1],
                         op0=ALU.mult,
                         op1=ALU.add,
                     )
@@ -345,8 +343,8 @@ def tile_styleganlayerepilogue_t_kernel(
                         out=yn,
                         in_=yn,
                         func=ACT.Identity,
-                        scale=a_t[:, n : n + 1],
-                        bias=b_t[:, n : n + 1],
+                        scale=a_t[:, k : k + 1],
+                        bias=b_t[:, k : k + 1],
                     )
 
         def t_back(g, h):
@@ -374,6 +372,17 @@ def tile_styleganlayerepilogue_t_kernel(
                 in_=o_sb[g][:].rearrange("p (j c) -> p j c", c=NF),
             )
 
+        def store_half(g, h):
+            ov = o_sb[g][:].rearrange("p (j c) -> p j c", c=NF)
+            dst = out_rows[GP * g : GP * (g + 1), :].rearrange("(j p) c -> p j c", j=4)
+            cols = slice(P * h, P * (h + 1))
+            nc.sync.dma_start(out=dst[:, :, cols], in_=ov[:, :, cols])
+
+        warm_ps = pso.tile([P, P], F32, name="warm_ps", tag="ot")
+        for rep in range(3):
+            nc.tensor.matmul(
+                out=warm_ps[:], lhsT=ident_f[:], rhs=ident_f[:], start=True, stop=True
+            )
         t_in(0, (0,))
         x_out(0, (0,))
         vectors()
@@ -405,61 +414,70 @@ def tile_styleganlayerepilogue_t_kernel(
             if i >= 1:
                 inv_std(i - 1)
                 add_noise(i, 0)
-            if i >= 1:
                 add_noise(i, 1)
-            if i >= 2:
-                for step in range(3):
-                    coefficient(i - 1, step, eng=nc.gpsimd)
-            if i == 0:
+            else:
                 lrelu(0, 0, GP)
                 lrelu(0, GP, 2 * GP)
             if i % 2 == 0 and i // 2 + 1 < NG // 2:
                 keep_noise(i // 2 + 1)
-            if i % 2 == 1 and i // 2 + 2 < NG // 2:
-                spread_noise(i // 2 + 2)
-            if i >= 2:
-                t_back(i - 2, 0)
-                t_back(i - 2, 1)
+            outgoing = [i - 3] if 3 <= i < NG - 1 else [NG - 4, NG - 3] if i == NG - 1 else []
+            for g in outgoing[:1]:
+                t_back(g, 0)
+                t_back(g, 1)
             if i + 1 < NG:
                 quant(i + 1)
                 products(i + 1, 0)
                 products(i + 1, 1)
             if i == 0:
                 style_copy()
+            if i % 2 == 1 and i // 2 + 2 < NG // 2:
+                spread_noise(i // 2 + 2)
             if i + 2 < NG:
                 x_out(i + 2)
-            if i >= 2:
-                copy_out(i - 2, 0, nc.scalar.copy)
-                copy_out(i - 2, 1, nc.scalar.copy)
-                store(i - 2)
+            for g in outgoing:
+                if g == NG - 3:
+                    t_back(g, 0)
+                    t_back(g, 1)
+                copy_out(g, 0, nc.scalar.copy)
+                copy_out(g, 1, nc.scalar.copy)
+                store(g)
+            if i == 1:
+                style_matmuls()
+                style_scales()
             if i + 3 < NG:
                 t_in(i + 3)
-            if i == 0:
-                style_matmuls()
-            if i == 1:
-                style_scales()
+            if i < NG - 3:
+                ready = (i // 2 - 1, 0, 32) if i % 2 == 0 and i >= 2 else None
+            else:
+                ready = ((i - 1) // 2, 16 * ((i - 1) % 2), 16 * ((i - 1) % 2) + 16)
+            if ready:
+                coefficient(ready[0], 0, ready[1], ready[2])
             if i >= 1:
                 lrelu(i, 0, GP)
-            if i >= 1:
+            if ready:
+                coefficient(ready[0], 1, ready[1], ready[2])
+                lrelu(i, GP, GP + half)
+                coefficient(ready[0], 2, ready[1], ready[2])
+                lrelu(i, GP + half, 2 * GP)
+            elif i >= 1:
                 lrelu(i, GP, 2 * GP)
             if i + 2 < NG:
                 noise(i + 2, 1)
                 noise(i + 2, 0)
-            if i >= 2:
-                affine(i - 1, 0, 16 if i < NG - 1 else 8, False)
-            moments(i, (0,))
-            moments(i, (1,))
-            if i == 1:
-                for step in range(3):
-                    coefficient(0, step)
-                affine(0, 0, 16, False)
+            if 2 <= i <= NG - 3:
+                affine(i - 2, 0, 16, False)
+            if NG - 3 <= i < NG - 1:
+                affine(i - 1, 0, 16, False)
+            if i == NG - 1:
+                affine(i - 1, 0, 8, False)
+            moments(i)
         g, z = NG - 2, NG - 1
         t_back(g, 0)
         affine(g, 8, 16, True)
         t_back(g, 1)
         inv_std(z)
         for step in range(3):
-            coefficient(z, step)
+            coefficient(z // 2, step, 16, 32)
         copy_out(g, 0, nc.scalar.copy)
         affine(z, 8, 16, True)
         affine(z, 0, 8, False)
@@ -467,6 +485,7 @@ def tile_styleganlayerepilogue_t_kernel(
         t_back(z, 0)
         copy_out(g, 1, nc.vector.tensor_copy)
         store(g)
-        copy_out(z, 0, nc.scalar.copy)
         copy_out(z, 1, nc.vector.tensor_copy)
-        store(z)
+        store_half(z, 1)
+        copy_out(z, 0, nc.scalar.copy)
+        store_half(z, 0)

@@ -17,6 +17,8 @@ CIN = 512
 NF = 256
 GP = 512
 NG = PIX // GP
+N_SPREAD = 6
+N_LEAD = 9
 EPS = 1e-8
 SLOPE = 0.2
 FLOPS = 2 * PIX * CIN * NF + 2 * 128 * 512 * 512
@@ -76,14 +78,15 @@ def tile_styleganlayerepilogue_t_kernel(
                 in_=x_rows[half * jj : half * (jj + 1), :].rearrange("(j p) k -> p j k", j=2),
             )
 
+        w_raw = const.tile([P, 4 * NF], BF16, name="w_raw")
+        nc.sync.dma_start(out=w_raw[:], in_=conv_w.rearrange("(i t) c -> i (t c)", t=4))
         load_x0(0)
         nc.sync.dma_start(out=rows[0:NG, :], in_=nm_flat.rearrange("(g n) -> g n", n=GP))
         nc.sync.dma_start(out=rows[16:17, 0:NF], in_=noise_weight.rearrange("a b c n -> (a b c) n"))
         nc.sync.dma_start(out=rows[16:17, NF : 2 * NF], in_=bias.rearrange("a b c n -> (a b c) n"))
         nc.sync.dma_start(out=rows[17:18, :], in_=dense_b.rearrange("(o n) -> o n", o=1))
-        w_raw = const.tile([P, 4 * NF], BF16, name="w_raw")
-        nc.sync.dma_start(out=w_raw[:], in_=conv_w.rearrange("(i t) c -> i (t c)", t=4))
         load_x0(1)
+        load_x(1)
         dl_sb = const.tile([P, 512], BF16, name="dl_sb")
         nc.sync.dma_start(out=dl_sb[:], in_=dlatents)
         dw_sb = const.tile([P, 2048], BF16, name="dw_sb")
@@ -91,7 +94,11 @@ def tile_styleganlayerepilogue_t_kernel(
             out=dw_sb[:].rearrange("p (kb n) -> p kb n", kb=4),
             in_=dense_w.rearrange("(kb p) n -> p kb n", p=P),
         )
-        for g in range(1, NG):
+        for g in range(2, N_LEAD):
+            load_x(g)
+        nm_late = const.tile([P, GP * (NG - N_SPREAD)], BF16, name="nm_late")
+        nc.sync.dma_start(out=nm_late[:], in_=nm_flat[GP * N_SPREAD :].partition_broadcast(P))
+        for g in range(N_LEAD, NG):
             load_x(g)
 
         w_grp = const.tile([P, 4 * NF], BF16, name="w_grp", align_bytes=64)
@@ -159,9 +166,13 @@ def tile_styleganlayerepilogue_t_kernel(
                     bias=b_col,
                 )
             else:
+                if g < N_SPREAD:
+                    src = nm_bc[g // 2][:].bitcast(BF16)[:, cols]
+                else:
+                    src = nm_late[:, GP * (g - N_SPREAD) : GP * (g - N_SPREAD + 1)]
                 nc.gpsimd.tensor_scalar(
                     out=dst,
-                    in0=nm_bc[g // 2][:].bitcast(BF16)[:, cols],
+                    in0=src,
                     scalar1=w_col,
                     scalar2=b_col,
                     op0=ALU.mult,
@@ -348,7 +359,8 @@ def tile_styleganlayerepilogue_t_kernel(
                     )
 
         def t_back(g, h):
-            ot = pso.tile([P, 512], F32, name="ot")
+            pool, tag = (psx, "xt") if g == NG - 1 else (pso, "ot")
+            ot = pool.tile([P, 512], F32, name="ot", tag=tag)
             for j in range(4):
                 nc.tensor.transpose(
                     ot[:, P * j : P * (j + 1)],
@@ -379,14 +391,14 @@ def tile_styleganlayerepilogue_t_kernel(
             nc.sync.dma_start(out=dst[:, :, cols], in_=ov[:, :, cols])
 
         warm_ps = pso.tile([P, P], F32, name="warm_ps", tag="ot")
-        for rep in range(3):
+        for rep in range(4):
             nc.tensor.matmul(
                 out=warm_ps[:], lhsT=ident_f[:], rhs=ident_f[:], start=True, stop=True
             )
+        quant_w()
         t_in(0, (0,))
         x_out(0, (0,))
         vectors()
-        quant_w()
         spread_noise(0)
         quant(0, 0, half)
         t_in(0, (1,))
@@ -397,9 +409,10 @@ def tile_styleganlayerepilogue_t_kernel(
         noise(0, 1, True)
         add_noise(0, 0, 0, half)
         quant(0, half, GP)
+        t_in(1, (0,))
         products(0, 0, half, GP)
         products(0, 1, half, GP)
-        t_in(1)
+        t_in(1, (1,))
         x_out(1)
         add_noise(0, 1, 0, half)
         add_noise(0, 0, half, GP)
@@ -418,7 +431,7 @@ def tile_styleganlayerepilogue_t_kernel(
             else:
                 lrelu(0, 0, GP)
                 lrelu(0, GP, 2 * GP)
-            if i % 2 == 0 and i // 2 + 1 < NG // 2:
+            if i % 2 == 0 and i // 2 + 1 < N_SPREAD // 2:
                 keep_noise(i // 2 + 1)
             outgoing = [i - 3] if 3 <= i < NG - 1 else [NG - 4, NG - 3] if i == NG - 1 else []
             for g in outgoing[:1]:
@@ -430,7 +443,7 @@ def tile_styleganlayerepilogue_t_kernel(
                 products(i + 1, 1)
             if i == 0:
                 style_copy()
-            if i % 2 == 1 and i // 2 + 2 < NG // 2:
+            if i % 2 == 1 and i // 2 + 2 < N_SPREAD // 2:
                 spread_noise(i // 2 + 2)
             if i + 2 < NG:
                 x_out(i + 2)
@@ -450,17 +463,22 @@ def tile_styleganlayerepilogue_t_kernel(
                 ready = (i // 2 - 1, 0, 32) if i % 2 == 0 and i >= 2 else None
             else:
                 ready = ((i - 1) // 2, 16 * ((i - 1) % 2), 16 * ((i - 1) % 2) + 16)
-            if ready:
+            if ready and i > 2:
                 coefficient(ready[0], 0, ready[1], ready[2])
             if i >= 1:
                 lrelu(i, 0, GP)
-            if ready:
+            if ready and i > 2:
                 coefficient(ready[0], 1, ready[1], ready[2])
+            if i == 2:
+                coefficient(0, 0)
                 lrelu(i, GP, GP + half)
-                coefficient(ready[0], 2, ready[1], ready[2])
+                coefficient(0, 1)
                 lrelu(i, GP + half, 2 * GP)
+                coefficient(0, 2)
             elif i >= 1:
                 lrelu(i, GP, 2 * GP)
+            if ready and i > 2:
+                coefficient(ready[0], 2, ready[1], ready[2])
             if i + 2 < NG:
                 noise(i + 2, 1)
                 noise(i + 2, 0)
@@ -469,13 +487,14 @@ def tile_styleganlayerepilogue_t_kernel(
             if NG - 3 <= i < NG - 1:
                 affine(i - 1, 0, 16, False)
             if i == NG - 1:
-                affine(i - 1, 0, 8, False)
+                affine(i - 1, 0, 4, False)
             moments(i)
         g, z = NG - 2, NG - 1
+        inv_std(z)
+        affine(g, 4, 8, False)
         t_back(g, 0)
         affine(g, 8, 16, True)
         t_back(g, 1)
-        inv_std(z)
         for step in range(3):
             coefficient(z // 2, step, 16, 32)
         copy_out(g, 0, nc.scalar.copy)

@@ -297,14 +297,32 @@ def tile_styleganlayerepilogue_t_kernel(
                 out=y_sb[g][:, cols], in0=zh, scalar=SLOPE, in1=zh, op0=ALU.mult, op1=ALU.max
             )
 
-        def moments(g):
+        def scalar_helps(g):
+            return g % 4 == 0 and g < NG - 4
+
+        def moments(g, pairs=range(8)):
             if g // 2 not in stats:
                 stats[g // 2] = spool.tile([P, 96], F32, name="st")
             st = stats[g // 2]
             yv = y_sb[g][:].rearrange("c (sp s2 q) -> c sp q s2", s2=2, q=64)
-            for sp in range(8):
+            for sp in pairs[:7] if scalar_helps(g) else pairs:
                 lo = 48 * (g % 2) + 6 * sp
                 nc.vector.bn_stats(out=st[:, lo : lo + 6], in_=yv[:, sp])
+
+        def moments_scalar(g):
+            st3 = stats[g // 2][:].rearrange("c (n k) -> c n k", k=3)
+            for k, func, scale in ((1, ACT.Identity, 1.0 / 64.0), (2, ACT.Square, -1.0)):
+                for n in (14, 15):
+                    col = 16 * (g % 2) + n
+                    junk = spool.tile([P, 64], F32, name="junk")
+                    nc.scalar.activation(
+                        out=junk[:],
+                        in_=y_sb[g][:, 64 * n : 64 * (n + 1)],
+                        func=func,
+                        scale=scale,
+                        bias=st3[:, col, 1:2] if k == 2 else 0.0,
+                        accum_out=st3[:, col, k : k + 1],
+                    )
 
         def inv_std(g):
             st3 = stats[g // 2][:].rearrange("c (n k) -> c n k", k=3)
@@ -359,8 +377,7 @@ def tile_styleganlayerepilogue_t_kernel(
                     )
 
         def t_back(g, h):
-            pool, tag = (psx, "xt") if g == NG - 1 else (pso, "ot")
-            ot = pool.tile([P, 512], F32, name="ot", tag=tag)
+            ot = pso.tile([P, 512], F32, name="ot")
             for j in range(4):
                 nc.tensor.transpose(
                     ot[:, P * j : P * (j + 1)],
@@ -384,11 +401,69 @@ def tile_styleganlayerepilogue_t_kernel(
                 in_=o_sb[g][:].rearrange("p (j c) -> p j c", c=NF),
             )
 
-        def store_half(g, h):
-            ov = o_sb[g][:].rearrange("p (j c) -> p j c", c=NF)
-            dst = out_rows[GP * g : GP * (g + 1), :].rearrange("(j p) c -> p j c", j=4)
-            cols = slice(P * h, P * (h + 1))
-            nc.sync.dma_start(out=dst[:, :, cols], in_=ov[:, :, cols])
+
+        def lrelu_part(g, part):
+            if g not in y_sb:
+                y_sb[g] = ypool.tile([P, 2 * GP], F32, name="y_sb")
+            cols = slice(half * part, half * (part + 1))
+            yp = y_sb[g][:].rearrange("c (h n) -> c h n", h=2)[:, :, cols]
+            zp = z_sb[g][:].rearrange("c (h n) -> c h n", h=2)[:, :, cols]
+            nc.vector.scalar_tensor_tensor(
+                out=yp, in0=zp, scalar=SLOPE, in1=zp, op0=ALU.mult, op1=ALU.max
+            )
+
+        def part_of(ap, part):
+            return ap.rearrange("c (e h p s) -> c e h p s", e=2, h=2, p=2)[:, 1, :, part, :]
+
+        def inv_std_part(g, part):
+            if g // 2 not in rstd:
+                rstd[g // 2] = spool.tile([P, 32], F32, name="rs")
+            dev = stats[g // 2][:].rearrange("c (n k) -> c n k", k=3)[:, :, 2]
+            nc.scalar.activation(
+                out=part_of(rstd[g // 2][:], part),
+                in_=part_of(dev, part),
+                func=ACT.Abs_reciprocal_sqrt,
+                scale=1.0 / 64.0,
+                bias=eps_t[:],
+            )
+
+        def coefficient_part(g, part, step):
+            a_t, b_t, ma = (part_of(t[:], part) for t in coef[g // 2])
+            mean = stats[g // 2][:].rearrange("c (n k) -> c n k", k=3)[:, :, 1]
+            cols = slice(32 * (g // 2), 32 * (g // 2 + 1))
+            out_t, in0, in1, op = (
+                (a_t, part_of(rstd[g // 2][:], part), part_of(g1[:, cols], part), ALU.mult),
+                (ma, part_of(mean, part), a_t, ALU.mult),
+                (b_t, part_of(bt[:, cols], part), ma, ALU.subtract),
+            )[step]
+            nc.vector.tensor_tensor(out=out_t, in0=in0, in1=in1, op=op)
+
+        def t_back_part(g, part):
+            for j in (2 * part, 2 * part + 1):
+                ot = (psp if part else psx).tile([P, GP], F32, name="ot", tag="acc" if part else "xt")
+                for h in range(2):
+                    nc.tensor.transpose(
+                        ot[:, P * h : P * (h + 1)],
+                        y_sb[g][:, GP * h + P * j : GP * h + P * (j + 1)],
+                        ident_f[:],
+                    )
+                outs[g, j] = ot
+
+        def copy_out_part(g, part):
+            if g not in o_sb:
+                o_sb[g] = opool.tile([P, 4 * NF], F32, name="o_sb")
+            j = 2 * part
+            nc.vector.tensor_copy(out=o_sb[g][:, NF * j : NF * (j + 1)], in_=outs[g, j][:, 0:NF])
+            j += 1
+            nc.scalar.copy(out=o_sb[g][:, NF * j : NF * (j + 1)], in_=outs[g, j][:, 0:NF])
+
+        def store_part(g, part):
+            nc.sync.dma_start(
+                out=out_rows[GP * g + half * part : GP * g + half * (part + 1), :].rearrange(
+                    "(j p) c -> p j c", j=2
+                ),
+                in_=o_sb[g][:, 2 * NF * part : 2 * NF * (part + 1)].rearrange("p (j c) -> p j c", c=NF),
+            )
 
         warm_ps = pso.tile([P, P], F32, name="warm_ps", tag="ot")
         for rep in range(4):
@@ -425,6 +500,8 @@ def tile_styleganlayerepilogue_t_kernel(
         t_in(2)
         for i in range(NG):
             if i >= 1:
+                if scalar_helps(i - 1):
+                    moments_scalar(i - 1)
                 inv_std(i - 1)
                 add_noise(i, 0)
                 add_noise(i, 1)
@@ -465,7 +542,9 @@ def tile_styleganlayerepilogue_t_kernel(
                 ready = ((i - 1) // 2, 16 * ((i - 1) % 2), 16 * ((i - 1) % 2) + 16)
             if ready and i > 2:
                 coefficient(ready[0], 0, ready[1], ready[2])
-            if i >= 1:
+            if i == NG - 1:
+                lrelu_part(i, 0)
+            elif i >= 1:
                 lrelu(i, 0, GP)
             if ready and i > 2:
                 coefficient(ready[0], 1, ready[1], ready[2])
@@ -475,6 +554,8 @@ def tile_styleganlayerepilogue_t_kernel(
                 coefficient(0, 1)
                 lrelu(i, GP + half, 2 * GP)
                 coefficient(0, 2)
+            elif i == NG - 1:
+                lrelu_part(i, 1)
             elif i >= 1:
                 lrelu(i, GP, 2 * GP)
             if ready and i > 2:
@@ -486,25 +567,33 @@ def tile_styleganlayerepilogue_t_kernel(
                 affine(i - 2, 0, 16, False)
             if NG - 3 <= i < NG - 1:
                 affine(i - 1, 0, 16, False)
-            if i == NG - 1:
-                affine(i - 1, 0, 4, False)
-            moments(i)
+            if i < NG - 1:
+                moments(i)
         g, z = NG - 2, NG - 1
-        inv_std(z)
-        affine(g, 4, 8, False)
+        moments(z, (0, 1, 4, 5))
+        inv_std_part(z, 0)
+        moments(z, (2, 3, 6, 7))
+        affine(g, 0, 8, False)
         t_back(g, 0)
-        affine(g, 8, 16, True)
+        inv_std_part(z, 1)
+        coefficient_part(z, 0, 0)
+        affine(g, 8, 12, True)
+        coefficient_part(z, 0, 1)
+        affine(g, 12, 16, True)
+        coefficient_part(z, 0, 2)
         t_back(g, 1)
-        for step in range(3):
-            coefficient(z // 2, step, 16, 32)
         copy_out(g, 0, nc.scalar.copy)
-        affine(z, 8, 16, True)
-        affine(z, 0, 8, False)
-        t_back(z, 1)
-        t_back(z, 0)
+        coefficient_part(z, 1, 0)
+        affine(z, 8, 12, True)
+        coefficient_part(z, 1, 1)
         copy_out(g, 1, nc.vector.tensor_copy)
         store(g)
-        copy_out(z, 1, nc.vector.tensor_copy)
-        store_half(z, 1)
-        copy_out(z, 0, nc.scalar.copy)
-        store_half(z, 0)
+        affine(z, 0, 4, False)
+        t_back_part(z, 0)
+        coefficient_part(z, 1, 2)
+        affine(z, 12, 16, True)
+        affine(z, 4, 8, False)
+        t_back_part(z, 1)
+        for part in range(2):
+            copy_out_part(z, part)
+            store_part(z, part)

from contextlib import ExitStack

import concourse.mybir as mybir
from concourse.masks import make_identity

F32 = mybir.dt.float32
BF16 = mybir.dt.bfloat16
U32 = mybir.dt.uint32
U8 = mybir.dt.uint8
FP8X4 = mybir.dt.float8_e4m3fn_x4
ALU = mybir.AluOpType
ACT = mybir.ActivationFunctionType

P = 128
PIX = 8192
CIN = 512
NF = 256
GP = 512
NG = PIX // GP
N_SPREAD = 6
N_LEAD = 9
EPS = 1e-8
SLOPE = 0.2
FLOPS = 2 * PIX * CIN * NF + 2 * 128 * 512 * 512


def tile_styleganlayerepilogue_t_kernel(
    tc, x, dlatents, noise_map, conv_w, noise_weight, bias, dense_w, dense_b, out
):
    nc = tc.nc
    x_rows = x.rearrange("b h w k -> (b h w) k")
    out_rows = out.rearrange("b h w c -> (b h w) c")
    nm_flat = noise_map.rearrange("b h w o -> (b h w o)")

    with ExitStack() as ctx:
        ctx.enter_context(tc.manual_schedule())
        const = ctx.enter_context(tc.tile_pool(name="const", bufs=1))
        xpool = ctx.enter_context(tc.tile_pool(name="xpool", bufs=NG))
        zpool = ctx.enter_context(tc.tile_pool(name="zpool", bufs=2))
        ypool = ctx.enter_context(tc.tile_pool(name="ypool", bufs=4))
        gpool = ctx.enter_context(tc.tile_pool(name="gpool", bufs=3))
        spool = ctx.enter_context(tc.tile_pool(name="spool", bufs=4))
        opool = ctx.enter_context(tc.tile_pool(name="opool", bufs=3))
        psx = ctx.enter_context(tc.psum_pool(name="psx", bufs=2))
        psp = ctx.enter_context(tc.psum_pool(name="psp", bufs=3))
        psn = ctx.enter_context(tc.psum_pool(name="psn", bufs=1))
        pso = ctx.enter_context(tc.psum_pool(name="pso", bufs=2))

        half = GP // 2

        ident_f = const.tile([P, P], F32, name="ident_f")
        make_identity(nc, ident_f[:])
        eps_t = const.tile([P, 1], F32, name="eps_t")
        nc.vector.memset(eps_t[:], EPS)
        rows = const.tile([P, GP], BF16, name="rows")
        nc.vector.memset(rows[:], 0.0)
        warm = const.tile([P, 1], F32, name="warm")
        nc.scalar.activation(out=warm[:], in_=eps_t[:], func=ACT.Abs_reciprocal_sqrt)
        ident_b = const.tile([P, P], BF16, name="ident_b")
        nc.vector.tensor_copy(out=ident_b[:], in_=ident_f[:])

        x_sb = []

        def load_x(g):
            t = xpool.tile([P, 4 * CIN], BF16, name="x_sb")
            nc.sync.dma_start(
                out=t[:].rearrange("p (j k) -> p j k", j=4),
                in_=x_rows[GP * g : GP * (g + 1), :].rearrange("(j p) k -> p j k", j=4),
            )
            x_sb.append(t)

        x_0 = xpool.tile([P, 4 * CIN], BF16, name="x_sb")
        x_sb.append(x_0)

        def load_x0(jj):
            nc.sync.dma_start(
                out=x_0[:, 2 * CIN * jj : 2 * CIN * (jj + 1)].rearrange("p (j k) -> p j k", j=2),
                in_=x_rows[half * jj : half * (jj + 1), :].rearrange("(j p) k -> p j k", j=2),
            )

        w_raw = const.tile([P, 4 * NF], BF16, name="w_raw")
        nc.sync.dma_start(out=w_raw[:], in_=conv_w.rearrange("(i t) c -> i (t c)", t=4))
        load_x0(0)
        nc.sync.dma_start(out=rows[0:NG, :], in_=nm_flat.rearrange("(g n) -> g n", n=GP))
        nc.sync.dma_start(out=rows[16:17, 0:NF], in_=noise_weight.rearrange("a b c n -> (a b c) n"))
        nc.sync.dma_start(out=rows[16:17, NF : 2 * NF], in_=bias.rearrange("a b c n -> (a b c) n"))
        nc.sync.dma_start(out=rows[17:18, :], in_=dense_b.rearrange("(o n) -> o n", o=1))
        load_x0(1)
        load_x(1)
        dl_sb = const.tile([P, 512], BF16, name="dl_sb")
        nc.sync.dma_start(out=dl_sb[:], in_=dlatents)
        dw_sb = const.tile([P, 2048], BF16, name="dw_sb")
        nc.sync.dma_start(
            out=dw_sb[:].rearrange("p (kb n) -> p kb n", kb=4),
            in_=dense_w.rearrange("(kb p) n -> p kb n", p=P),
        )
        for g in range(2, N_LEAD):
            load_x(g)
        nm_late = const.tile([P, GP * (NG - N_SPREAD)], BF16, name="nm_late")
        nc.sync.dma_start(out=nm_late[:], in_=nm_flat[GP * N_SPREAD :].partition_broadcast(P))
        for g in range(N_LEAD, NG):
            load_x(g)

        w_grp = const.tile([P, 4 * NF], BF16, name="w_grp", align_bytes=64)
        w_codes = const.tile([P, NF], U32, name="w_codes", align_bytes=64)
        w_scl = const.tile([P, NF], U8, name="w_scl", align_bytes=64)

        def quant_w():
            nc.vector.tensor_copy(
                out=w_grp[:].rearrange("i (c t) -> i c t", t=4),
                in_=w_raw[:].rearrange("i (t c) -> i c t", t=4),
            )
            nc.vector.quantize_mx(out=w_codes[:].bitcast(FP8X4), scales=w_scl[:], in_=w_grp[:])

        vec = const.tile([P, 8], F32, name="vec")
        vec3 = vec[:].rearrange("c (b r) -> c b r", r=2)
        one_g = const.tile([P, 2], F32, name="one_g")
        nm_pix = const.tile([P, 2, NG], F32, name="nm_pix")

        def vectors():
            nps = pso.tile([P, 2, P], F32, name="nps", tag="ot")
            vps = pso.tile([P, 4, P], BF16, name="vps", tag="ot")
            rows_32 = rows[:].bitcast(F32)
            for jj in range(2):
                nc.tensor.transpose(nps[:, jj, :], rows_32[:, P * jj : P * (jj + 1)], ident_f[:])
            for b in range(4):
                nc.tensor.transpose(vps[:, b, :], rows[:, P * b : P * (b + 1)], ident_b[:])
            nc.vector.tensor_copy(out=nm_pix[:], in_=nps[:, :, 0:NG])
            nc.vector.tensor_copy(out=vec3, in_=vps[:, :, 16:18])

        nm_ps = {}
        nm_bc = {}

        def spread_noise(q):
            nb = (pso if q == 1 else psn).tile([P, GP], F32, name="nb", tag="ot" if q == 1 else "nb")
            for e in range(2):
                for jj in range(2):
                    lo = half * e + P * jj
                    nc.tensor.transpose(
                        nb[:, lo : lo + P],
                        nm_pix[:, jj, 2 * q + e : 2 * q + e + 1].to_broadcast([P, P]),
                        ident_f[:],
                    )
            nm_ps[q] = nb

        def keep_noise(q):
            t = const.tile([P, GP], F32, name="nm_bc%d" % q)
            nc.scalar.copy(out=t[:], in_=nm_ps[q][:])
            nm_bc[q] = t

        z_sb = {}
        y_sb = {}

        def noise(g, h, on_scalar=False):
            if g not in z_sb:
                z_sb[g] = zpool.tile([P, 2 * GP], F32, name="z_sb")
            dst = z_sb[g][:, GP * h : GP * (h + 1)]
            cols = slice(GP * (g % 2), GP * (g % 2 + 1))
            w_col, b_col = vec3[:, h, 0:1], vec3[:, 2 + h, 0:1]
            if on_scalar:
                nc.scalar.activation(
                    out=dst,
                    in_=nm_ps[g // 2][:].bitcast(BF16)[:, cols],
                    func=ACT.Identity,
                    scale=w_col,
                    bias=b_col,
                )
            else:
                if g < N_SPREAD:
                    src = nm_bc[g // 2][:].bitcast(BF16)[:, cols]
                else:
                    src = nm_late[:, GP * (g - N_SPREAD) : GP * (g - N_SPREAD + 1)]
                nc.gpsimd.tensor_scalar(
                    out=dst,
                    in0=src,
                    scalar1=w_col,
                    scalar2=b_col,
                    op0=ALU.mult,
                    op1=ALU.add,
                )

        g1 = const.tile([P, 2 * P], F32, name="g1")
        bt = const.tile([P, 2 * P], F32, name="bt")
        dl_t = const.tile([P, 512], BF16, name="dl_t")
        style_ps = {}

        def style_transposes():
            dl_ps = pso.tile([P, 512], BF16, name="dl_ps", tag="ot")
            for kb in range(4):
                nc.tensor.transpose(
                    dl_ps[:, P * kb : P * (kb + 1)], dl_sb[:, P * kb : P * (kb + 1)], ident_b[:]
                )
            style_ps["dl"] = dl_ps

        def style_copy():
            nc.vector.tensor_copy(out=dl_t[:], in_=style_ps["dl"][:])

        def style_matmuls():
            gb = pso.tile([P, 512], F32, name="gb", tag="ot")
            for cb in range(4):
                for kb in range(4):
                    nc.tensor.matmul(
                        out=gb[:, P * cb : P * (cb + 1)],
                        lhsT=dw_sb[:, 512 * kb + P * cb : 512 * kb + P * (cb + 1)],
                        rhs=dl_t[:, P * kb : P * (kb + 1)],
                        start=(kb == 0),
                        stop=(kb == 3),
                    )
            style_ps["gb"] = gb

        def style_scales():
            gb = style_ps["gb"]
            g1v = g1[:].rearrange("c (g h s) -> c h g s", h=2, s=8)
            btv = bt[:].rearrange("c (g h s) -> c h g s", h=2, s=8)
            for h in range(2):
                nc.scalar.activation(
                    out=g1v[:, h],
                    in_=gb[:, P * h : P * (h + 1)].rearrange("c (g s) -> c g s", s=8),
                    func=ACT.Identity,
                    bias=one_g[:, h : h + 1],
                )
                nc.scalar.activation(
                    out=btv[:, h],
                    in_=gb[:, P * (2 + h) : P * (3 + h)].rearrange("c (g s) -> c g s", s=8),
                    func=ACT.Identity,
                    bias=vec3[:, 2 + h, 1:2],
                )

        xts = {}
        grp = {}
        codes = {}
        prod = {}
        outs = {}
        o_sb = {}
        stats = {}
        rstd = {}
        coef = {}

        def t_in(g, parts=(0, 1)):
            x32 = x_sb[g][:].bitcast(F32)
            for jj in parts:
                xt = psx.tile([P, 512], F32, name="xt")
                for u in range(2):
                    for j2 in range(2):
                        j = 2 * jj + j2
                        nc.tensor.transpose(
                            xt[:, 256 * u + P * j2 : 256 * u + P * (j2 + 1)],
                            x32[:, 256 * j + u : 256 * (j + 1) : 2],
                            ident_f[:],
                        )
                xts[g, jj] = xt

        def x_out(g, parts=(0, 1)):
            if g not in grp:
                grp[g] = gpool.tile([P, 4 * GP], BF16, name="grp", align_bytes=64)
            t32 = grp[g][:].bitcast(F32)
            for jj in parts:
                nc.scalar.copy(
                    out=t32[:, 512 * jj : 512 * (jj + 1)].rearrange("p (c u) -> p c u", u=2),
                    in_=xts[g, jj][:].rearrange("p (u c) -> p c u", u=2),
                )

        def quant(g, lo=0, hi=GP):
            if g not in codes:
                cd = gpool.tile([P, GP], U32, name="codes", align_bytes=64)
                sc = gpool.tile([P, GP], U8, name="scl", align_bytes=64)
                codes[g] = (cd, sc)
            cd, sc = codes[g]
            nc.vector.quantize_mx(
                out=cd[:, lo:hi].bitcast(FP8X4), scales=sc[:, lo:hi], in_=grp[g][:, 4 * lo : 4 * hi]
            )

        def products(g, h, lo=0, hi=GP):
            cd, sc = codes[g]
            if (g, h) not in prod:
                prod[g, h] = psp.tile([P, GP], F32, name="acc")
            nc.tensor.matmul_mx(
                out=prod[g, h][:, lo:hi],
                lhsT=w_codes[:, P * h : P * (h + 1)].bitcast(FP8X4),
                lhsT_scale=w_scl[:, P * h : P * (h + 1)],
                rhs=cd[:, lo:hi].bitcast(FP8X4),
                rhs_scale=sc[:, lo:hi],
                start=True,
                stop=True,
            )

        def add_noise(g, h, lo=0, hi=GP):
            zc = z_sb[g][:, GP * h + lo : GP * h + hi]
            nc.vector.tensor_tensor(out=zc, in0=prod[g, h][:, lo:hi], in1=zc, op=ALU.add)

        def lrelu(g, lo, hi):
            if g not in y_sb:
                y_sb[g] = ypool.tile([P, 2 * GP], F32, name="y_sb")
            cols = slice(lo, hi)
            zh = z_sb[g][:, cols]
            nc.vector.scalar_tensor_tensor(
                out=y_sb[g][:, cols], in0=zh, scalar=SLOPE, in1=zh, op0=ALU.mult, op1=ALU.max
            )

        def scalar_helps(g):
            return g % 4 == 0 and g < NG - 4

        def moments(g, pairs=range(8)):
            if g // 2 not in stats:
                stats[g // 2] = spool.tile([P, 96], F32, name="st")
            st = stats[g // 2]
            yv = y_sb[g][:].rearrange("c (sp s2 q) -> c sp q s2", s2=2, q=64)
            for sp in pairs[:7] if scalar_helps(g) else pairs:
                lo = 48 * (g % 2) + 6 * sp
                nc.vector.bn_stats(out=st[:, lo : lo + 6], in_=yv[:, sp])

        def moments_scalar(g):
            st3 = stats[g // 2][:].rearrange("c (n k) -> c n k", k=3)
            for k, func, scale in ((1, ACT.Identity, 1.0 / 64.0), (2, ACT.Square, -1.0)):
                for n in (14, 15):
                    col = 16 * (g % 2) + n
                    junk = spool.tile([P, 64], F32, name="junk")
                    nc.scalar.activation(
                        out=junk[:],
                        in_=y_sb[g][:, 64 * n : 64 * (n + 1)],
                        func=func,
                        scale=scale,
                        bias=st3[:, col, 1:2] if k == 2 else 0.0,
                        accum_out=st3[:, col, k : k + 1],
                    )

        def inv_std(g):
            st3 = stats[g // 2][:].rearrange("c (n k) -> c n k", k=3)
            if g // 2 not in rstd:
                rstd[g // 2] = spool.tile([P, 32], F32, name="rs")
            cols = slice(16 * (g % 2), 16 * (g % 2 + 1))
            nc.scalar.activation(
                out=rstd[g // 2][:, cols],
                in_=st3[:, cols, 2],
                func=ACT.Abs_reciprocal_sqrt,
                scale=1.0 / 64.0,
                bias=eps_t[:],
            )

        def coefficient(q, step, lo=0, hi=32):
            if q not in coef:
                a_t = spool.tile([P, 32], F32, name="a_t")
                b_t = spool.tile([P, 32], F32, name="b_t")
                ma = spool.tile([P, 32], F32, name="ma")
                coef[q] = (a_t, b_t, ma)
            a_t, b_t, ma = coef[q]
            cols = slice(32 * q + lo, 32 * q + hi)
            mean = stats[q][:].rearrange("c (n k) -> c n k", k=3)[:, lo:hi, 1]
            out_t, in0, in1, op = (
                (a_t, rstd[q][:, lo:hi], g1[:, cols], ALU.mult),
                (ma, mean, a_t[:, lo:hi], ALU.mult),
                (b_t, bt[:, cols], ma[:, lo:hi], ALU.subtract),
            )[step]
            nc.vector.tensor_tensor(out=out_t[:, lo:hi], in0=in0, in1=in1, op=op)

        def affine(g, lo, hi, on_vector):
            a_t, b_t, ma = coef[g // 2]
            for n in range(lo, hi):
                yn = y_sb[g][:, 64 * n : 64 * (n + 1)]
                k = 16 * (g % 2) + n
                if on_vector:
                    nc.vector.tensor_scalar(
                        out=yn,
                        in0=yn,
                        scalar1=a_t[:, k : k + 1],
                        scalar2=b_t[:, k : k + 1],
                        op0=ALU.mult,
                        op1=ALU.add,
                    )
                else:
                    nc.scalar.activation(
                        out=yn,
                        in_=yn,
                        func=ACT.Identity,
                        scale=a_t[:, k : k + 1],
                        bias=b_t[:, k : k + 1],
                    )

        def t_back(g, h):
            ot = pso.tile([P, 512], F32, name="ot")
            for j in range(4):
                nc.tensor.transpose(
                    ot[:, P * j : P * (j + 1)],
                    y_sb[g][:, GP * h + P * j : GP * h + P * (j + 1)],
                    ident_f[:],
                )
            outs[g, h] = ot

        def copy_out(g, h, eng_copy):
            if g not in o_sb:
                o_sb[g] = opool.tile([P, 4 * NF], F32, name="o_sb")
            ov = o_sb[g][:].rearrange("p (j c) -> p j c", c=NF)
            eng_copy(
                out=ov[:, :, P * h : P * (h + 1)],
                in_=outs[g, h][:].rearrange("p (j c) -> p j c", c=P),
            )

        def store(g):
            nc.sync.dma_start(
                out=out_rows[GP * g : GP * (g + 1), :].rearrange("(j p) c -> p j c", j=4),
                in_=o_sb[g][:].rearrange("p (j c) -> p j c", c=NF),
            )


        def lrelu_part(g, part):
            if g not in y_sb:
                y_sb[g] = ypool.tile([P, 2 * GP], F32, name="y_sb")
            cols = slice(half * part, half * (part + 1))
            yp = y_sb[g][:].rearrange("c (h n) -> c h n", h=2)[:, :, cols]
            zp = z_sb[g][:].rearrange("c (h n) -> c h n", h=2)[:, :, cols]
            nc.vector.scalar_tensor_tensor(
                out=yp, in0=zp, scalar=SLOPE, in1=zp, op0=ALU.mult, op1=ALU.max
            )

        def part_of(ap, part):
            return ap.rearrange("c (e h p s) -> c e h p s", e=2, h=2, p=2)[:, 1, :, part, :]

        def inv_std_part(g, part):
            if g // 2 not in rstd:
                rstd[g // 2] = spool.tile([P, 32], F32, name="rs")
            dev = stats[g // 2][:].rearrange("c (n k) -> c n k", k=3)[:, :, 2]
            nc.scalar.activation(
                out=part_of(rstd[g // 2][:], part),
                in_=part_of(dev, part),
                func=ACT.Abs_reciprocal_sqrt,
                scale=1.0 / 64.0,
                bias=eps_t[:],
            )

        def coefficient_part(g, part, step):
            a_t, b_t, ma = (part_of(t[:], part) for t in coef[g // 2])
            mean = stats[g // 2][:].rearrange("c (n k) -> c n k", k=3)[:, :, 1]
            cols = slice(32 * (g // 2), 32 * (g // 2 + 1))
            out_t, in0, in1, op = (
                (a_t, part_of(rstd[g // 2][:], part), part_of(g1[:, cols], part), ALU.mult),
                (ma, part_of(mean, part), a_t, ALU.mult),
                (b_t, part_of(bt[:, cols], part), ma, ALU.subtract),
            )[step]
            nc.vector.tensor_tensor(out=out_t, in0=in0, in1=in1, op=op)

        def t_back_part(g, part):
            for j in (2 * part, 2 * part + 1):
                ot = (psp if part else psx).tile([P, GP], F32, name="ot", tag="acc" if part else "xt")
                for h in range(2):
                    nc.tensor.transpose(
                        ot[:, P * h : P * (h + 1)],
                        y_sb[g][:, GP * h + P * j : GP * h + P * (j + 1)],
                        ident_f[:],
                    )
                outs[g, j] = ot

        def copy_out_part(g, part):
            if g not in o_sb:
                o_sb[g] = opool.tile([P, 4 * NF], F32, name="o_sb")
            j = 2 * part
            nc.vector.tensor_copy(out=o_sb[g][:, NF * j : NF * (j + 1)], in_=outs[g, j][:, 0:NF])
            j += 1
            nc.scalar.copy(out=o_sb[g][:, NF * j : NF * (j + 1)], in_=outs[g, j][:, 0:NF])

        def store_part(g, part):
            nc.sync.dma_start(
                out=out_rows[GP * g + half * part : GP * g + half * (part + 1), :].rearrange(
                    "(j p) c -> p j c", j=2
                ),
                in_=o_sb[g][:, 2 * NF * part : 2 * NF * (part + 1)].rearrange("p (j c) -> p j c", c=NF),
            )

        warm_ps = pso.tile([P, P], F32, name="warm_ps", tag="ot")
        for rep in range(4):
            nc.tensor.matmul(
                out=warm_ps[:], lhsT=ident_f[:], rhs=ident_f[:], start=True, stop=True
            )
        quant_w()
        t_in(0, (0,))
        x_out(0, (0,))
        vectors()
        spread_noise(0)
        quant(0, 0, half)
        t_in(0, (1,))
        noise(0, 0, True)
        products(0, 0, 0, half)
        products(0, 1, 0, half)
        x_out(0, (1,))
        noise(0, 1, True)
        add_noise(0, 0, 0, half)
        quant(0, half, GP)
        t_in(1, (0,))
        products(0, 0, half, GP)
        products(0, 1, half, GP)
        t_in(1, (1,))
        x_out(1)
        add_noise(0, 1, 0, half)
        add_noise(0, 0, half, GP)
        add_noise(0, 1, half, GP)
        noise(1, 0, True)
        noise(1, 1, True)
        spread_noise(1)
        style_transposes()
        nc.vector.tensor_scalar_add(out=one_g[:], in0=vec3[:, 0:2, 1], scalar1=1.0)
        t_in(2)
        for i in range(NG):
            if i >= 1:
                if scalar_helps(i - 1):
                    moments_scalar(i - 1)
                inv_std(i - 1)
                add_noise(i, 0)
                add_noise(i, 1)
            else:
                lrelu(0, 0, GP)
                lrelu(0, GP, 2 * GP)
            if i % 2 == 0 and i // 2 + 1 < N_SPREAD // 2:
                keep_noise(i // 2 + 1)
            outgoing = [i - 3] if 3 <= i < NG - 1 else [NG - 4, NG - 3] if i == NG - 1 else []
            for g in outgoing[:1]:
                t_back(g, 0)
                t_back(g, 1)
            if i + 1 < NG:
                quant(i + 1)
                products(i + 1, 0)
                products(i + 1, 1)
            if i == 0:
                style_copy()
            if i % 2 == 1 and i // 2 + 2 < N_SPREAD // 2:
                spread_noise(i // 2 + 2)
            if i + 2 < NG:
                x_out(i + 2)
            for g in outgoing:
                if g == NG - 3:
                    t_back(g, 0)
                    t_back(g, 1)
                copy_out(g, 0, nc.scalar.copy)
                copy_out(g, 1, nc.scalar.copy)
                store(g)
            if i == 1:
                style_matmuls()
                style_scales()
            if i + 3 < NG:
                t_in(i + 3)
            if i < NG - 3:
                ready = (i // 2 - 1, 0, 32) if i % 2 == 0 and i >= 2 else None
            else:
                ready = ((i - 1) // 2, 16 * ((i - 1) % 2), 16 * ((i - 1) % 2) + 16)
            if ready and i > 2:
                coefficient(ready[0], 0, ready[1], ready[2])
            if i == NG - 1:
                lrelu_part(i, 0)
            elif i >= 1:
                lrelu(i, 0, GP)
            if ready and i > 2:
                coefficient(ready[0], 1, ready[1], ready[2])
            if i == 2:
                coefficient(0, 0)
                lrelu(i, GP, GP + half)
                coefficient(0, 1)
                lrelu(i, GP + half, 2 * GP)
                coefficient(0, 2)
            elif i == NG - 1:
                lrelu_part(i, 1)
            elif i >= 1:
                lrelu(i, GP, 2 * GP)
            if ready and i > 2:
                coefficient(ready[0], 2, ready[1], ready[2])
            if i + 2 < NG:
                noise(i + 2, 1)
                noise(i + 2, 0)
            if 2 <= i <= NG - 3:
                affine(i - 2, 0, 16, False)
            if NG - 3 <= i < NG - 1:
                affine(i - 1, 0, 16, False)
            if i < NG - 1:
                moments(i)
        g, z = NG - 2, NG - 1
        moments(z, (0, 1, 4, 5))
        inv_std_part(z, 0)
        moments(z, (2, 3, 6, 7))
        affine(g, 0, 8, False)
        t_back(g, 0)
        inv_std_part(z, 1)
        coefficient_part(z, 0, 0)
        affine(g, 8, 12, True)
        coefficient_part(z, 0, 1)
        affine(g, 12, 16, True)
        coefficient_part(z, 0, 2)
        t_back(g, 1)
        copy_out(g, 0, nc.scalar.copy)
        coefficient_part(z, 1, 0)
        affine(z, 8, 12, True)
        coefficient_part(z, 1, 1)
        copy_out(g, 1, nc.vector.tensor_copy)
        store(g)
        affine(z, 0, 4, False)
        t_back_part(z, 0)
        coefficient_part(z, 1, 2)
        affine(z, 12, 16, True)
        affine(z, 4, 8, False)
        t_back_part(z, 1)
        for part in range(2):
            copy_out_part(z, part)
            store_part(z, part)
